import numpy as np
import ml_dtypes


def mxq(x, axis, fmt="e4m3"):
    dtype, down = {"e4m3": (ml_dtypes.float8_e4m3fn, 7), "e5m2": (ml_dtypes.float8_e5m2, 14)}[fmt]
    v = np.moveaxis(np.asarray(x, np.float32).astype(ml_dtypes.bfloat16).astype(np.float64), axis, -1)
    blocks = v.reshape(v.shape[:-1] + (-1, 32))
    amax = np.abs(blocks).max(-1, keepdims=True)
    byte = np.maximum(np.where(amax > 0, np.frexp(amax)[1] - 1 + 127, 0) - down, 1)
    scale = np.exp2(byte - 127.0)
    codes = (blocks / scale).astype(np.float32).astype(dtype).astype(np.float64)
    return np.moveaxis((codes * scale).reshape(v.shape), -1, axis)


WIDE = False


def mx_kscale(k):
    if not WIDE:
        return np.ones(k)
    levels = np.array([10, -10, 5, -5, 0])
    a = np.random.permutation(np.resize(levels, k // 512 * 4)).reshape(k // 512, 4)
    idx = np.arange(k)
    return np.exp2(a[idx // 512, idx % 128 // 32])


BF16 = ml_dtypes.bfloat16


def bf(x):
    return np.asarray(x, np.float32).astype(BF16)


def f64(x):
    return np.asarray(x).astype(np.float64)


B, S, I, K, O = 128, 32, 512, 2, 128


def setup_inputs():
    t = np.exp2(np.round(np.log2(mx_kscale(K * I)[:I]) / K))
    tp = t[:, None] ** np.arange(1, K + 1)
    return {"x": bf(np.random.standard_normal((B, S, I)) * t),
            "taylor_a_0_1": bf(np.random.standard_normal((1, S, I, K, O)) / np.sqrt(K * I) / tp[:, :, None]),
            "taylor_a_0": bf(np.random.standard_normal((1, S, I, O)) / np.sqrt(I))}


def reference(x, taylor_a_0_1, taylor_a_0):
    powers = f64(x)[..., None] ** np.arange(1, K + 1)
    p = powers.transpose(1, 0, 3, 2).reshape(S, B, K * I)
    a = f64(taylor_a_0_1)[0].transpose(0, 2, 1, 3).reshape(S, K * I, O)
    out = (mxq(p, 2, "e4m3") @ mxq(a, 1, "e4m3")).transpose(1, 0, 2)
    return out + np.sum(f64(taylor_a_0), axis=2)

@@ -1,0 +1,166 @@
+from contextlib import ExitStack
+
+import concourse.mybir as mybir
+from concourse.masks import make_identity
+
+F32 = mybir.dt.float32
+BF16 = mybir.dt.bfloat16
+U32 = mybir.dt.uint32
+U8 = mybir.dt.uint8
+FP8X4 = mybir.dt.float8_e4m3fn_x4
+ADD = mybir.AluOpType.add
+SQUARE = mybir.ActivationFunctionType.Square
+AXIS_X = mybir.AxisListType.X
+
+P = 128
+B = 128
+S = 32
+I = 512
+NPOW = 2
+O = 128
+PACK = 4
+G = 4
+NG = S // G
+ROWS = G * I // P
+
+FLOPS = 2 * B * S * NPOW * I * O
+
+SCALAR_GROUPS = (0, 2, 3, 5, 6)
+
+
+def tile_modelsingle_kernel(tc, x, taylor_a_0_1, taylor_a_0, out):
+    nc = tc.nc
+    with ExitStack() as ctx:
+        const = ctx.enter_context(tc.tile_pool(name="const", bufs=1))
+        loads = ctx.enter_context(tc.tile_pool(name="loads", bufs=NG))
+        work = ctx.enter_context(tc.tile_pool(name="work", bufs=3))
+        quant = ctx.enter_context(tc.tile_pool(name="quant", bufs=2))
+        small = ctx.enter_context(tc.tile_pool(name="small", bufs=3))
+        psum = ctx.enter_context(tc.psum_pool(name="psum", bufs=2))
+
+        a0_rows = taylor_a_0.rearrange("u s i o -> (u s i) o")
+        x_in = []
+        w_in = []
+        z_in = []
+        for g in range(NG):
+            s0 = g * G
+            xs = loads.tile([P, G * I], BF16)
+            nc.sync.dma_start(out=xs[:], in_=x[:, s0:s0 + G, :].rearrange("b s i -> b (s i)"))
+            ws = loads.tile([P, G, PACK * NPOW * O], BF16)
+            nc.sync.dma_start(
+                out=ws[:],
+                in_=taylor_a_0_1[0, s0:s0 + G].rearrange("s (p j) w o -> p s (j w o)", j=PACK),
+            )
+            zs = loads.tile([P, ROWS * O], BF16)
+            nc.sync.dma_start(
+                out=zs[:],
+                in_=a0_rows[s0 * I:(s0 + G) * I, :].rearrange("(p r) o -> p (r o)", r=ROWS),
+            )
+            x_in.append(xs)
+            w_in.append(ws)
+            z_in.append(zs)
+
+        ident = const.tile([P, P], F32)
+        make_identity(nc, ident[:])
+        sel_f = const.tile([P, G], F32)
+        nc.vector.tensor_reduce(
+            out=sel_f[:], in_=ident[:].rearrange("p (c r) -> p c r", c=G), axis=AXIS_X, op=ADD
+        )
+        sel = const.tile([P, G], BF16)
+        nc.vector.tensor_copy(out=sel[:], in_=sel_f[:])
+
+        grouped = {}
+        biases = {}
+
+        def prepare(g):
+            xw = x_in[g][:].bitcast(F32).rearrange("b (s p u) -> b s u p", s=G, u=2)
+            xg = work.tile([P, NPOW * G * B * PACK], BF16, align_bytes=64)
+            xg_words = xg[:].bitcast(F32).rearrange(
+                "p (w h c u) -> p w h c u", w=NPOW, h=G // 2, u=2
+            )
+            xg_vals = xg[:].rearrange(
+                "p (w h c u e) -> p w h c u e", w=NPOW, h=G // 2, u=2, e=2
+            )
+            for h in range(G // 2):
+                xt = psum.tile([P, 4 * B], F32, tag="xt")
+                for u in range(2):
+                    for sl in range(2):
+                        col = (u * 2 + sl) * B
+                        nc.tensor.transpose(
+                            out=xt[:, col:col + B], in_=xw[:, 2 * h + sl, u, :], identity=ident[:]
+                        )
+                nc.scalar.copy(
+                    out=xg_words[:, 0, h], in_=xt[:].rearrange("p (u c) -> p c u", u=2)
+                )
+                nc.scalar.activation(
+                    out=xg_vals[:, 1, h],
+                    in_=xt[:].bitcast(BF16).rearrange("p (u c e) -> p c u e", u=2, e=2),
+                    func=SQUARE,
+                )
+
+            ag = work.tile([P, G * NPOW * O * PACK], BF16, align_bytes=64)
+            src = w_in[g][:].rearrange("p s (t c i) -> p s c t i", t=PACK, i=4)
+            dst = ag[:].rearrange("p (s c i t) -> p s c t i", s=G, i=4, t=PACK)
+            nc.vector.tensor_copy(out=dst[:, 0:2], in_=src[:, 0:2])
+            if g in SCALAR_GROUPS:
+                nc.vector.tensor_copy(out=dst[:, 2], in_=src[:, 2])
+                nc.scalar.copy(out=dst[:, 3], in_=src[:, 3])
+            else:
+                nc.vector.tensor_copy(out=dst[:, 2:4], in_=src[:, 2:4])
+            grouped[g] = (xg, ag)
+
+            bsum = psum.tile([P, G], F32, tag="bsum", bufs=1)
+            for r in range(ROWS):
+                nc.tensor.matmul(
+                    out=bsum[:],
+                    lhsT=z_in[g][:, r * O:(r + 1) * O],
+                    rhs=sel[:],
+                    start=(r == 0),
+                    stop=(r == ROWS - 1),
+                )
+            bcol = small.tile([P, G], F32)
+            nc.scalar.copy(out=bcol[:], in_=bsum[:])
+            bb = psum.tile([P, G * O], F32, tag="bb")
+            for c in range(G):
+                nc.tensor.transpose(
+                    out=bb[:, c * O:(c + 1) * O],
+                    in_=bcol[:, c:c + 1].to_broadcast([P, P]),
+                    identity=ident[:],
+                )
+            bias = small.tile([P, G * O], F32)
+            nc.scalar.copy(out=bias[:], in_=bb[:])
+            biases[g] = bias
+
+        def multiply(g):
+            xg, ag = grouped[g]
+            a_codes = quant.tile([P, G * NPOW * O], U32, align_bytes=64)
+            a_scales = quant.tile([P, G * NPOW * O], U8, align_bytes=64)
+            nc.vector.quantize_mx(out=a_codes[:].bitcast(FP8X4), scales=a_scales[:], in_=ag[:])
+            x_codes = quant.tile([P, NPOW * G * B], U32, align_bytes=64)
+            x_scales = quant.tile([P, NPOW * G * B], U8, align_bytes=64)
+            nc.vector.quantize_mx(out=x_codes[:].bitcast(FP8X4), scales=x_scales[:], in_=xg[:])
+            acc = psum.tile([P, G * O], F32, tag="acc")
+            for s in range(G):
+                for w in range(NPOW):
+                    xc = (w * G + s) * B
+                    ac = (s * NPOW + w) * O
+                    nc.tensor.matmul_mx(
+                        out=acc[:, s * O:(s + 1) * O],
+                        lhsT=x_codes[:, xc:xc + B].bitcast(FP8X4),
+                        lhsT_scale=x_scales[:, xc:xc + B],
+                        rhs=a_codes[:, ac:ac + O].bitcast(FP8X4),
+                        rhs_scale=a_scales[:, ac:ac + O],
+                        start=(w == 0),
+                        stop=(w == NPOW - 1),
+                    )
+            res = small.tile([P, G * O], F32)
+            nc.vector.tensor_tensor(out=res[:], in0=acc[:], in1=biases[g][:], op=ADD)
+            nc.sync.dma_start(
+                out=out[:, g * G:(g + 1) * G, :].rearrange("b s o -> b (s o)"), in_=res[:]
+            )
+
+        prepare(0)
+        for g in range(1, NG):
+            prepare(g)
+            multiply(g - 1)
+        multiply(NG - 1)

@@ -25,40 +25,47 @@ ROWS = G * I // P
 
 FLOPS = 2 * B * S * NPOW * I * O
 
-SCALAR_GROUPS = (0, 2, 3, 5, 6)
+MANUAL = True
+W_SIZES = (2, 2, 2, 2, 4, 4, 4, 4, 4, 2, 1, 1)
+X_SIZES = (2, 2, 4, 4, 4, 4, 4, 4, 4)
+SCALAR_S = (11, 15, 19, 23, 27, 31)
+
+
+def starts(sizes):
+    res = []
+    s0 = 0
+    for n in sizes:
+        res.append((s0, n))
+        s0 += n
+    return res
 
 
 def tile_modelsingle_kernel(tc, x, taylor_a_0_1, taylor_a_0, out):
     nc = tc.nc
+    wch = starts(W_SIZES)
+    xch = starts(X_SIZES)
+    nw = len(wch)
+    w_at = dict((s0, k) for k, (s0, n) in enumerate(wch))
+    x_tied = dict((w_at[s0], j) for j, (s0, n) in enumerate(xch))
+    x_of_s = {}
+    for j, (s0, n) in enumerate(xch):
+        for sl in range(n):
+            x_of_s[s0 + sl] = (j, sl, n)
+    zit = dict((z + 2, z) for z in range(NG))
+    dit = {}
+    for c, (s0, n) in enumerate(wch):
+        k = max(c + 1, s0 // G + 3)
+        dit[k] = dit.get(k, []) + [c]
+
     with ExitStack() as ctx:
+        if MANUAL:
+            ctx.enter_context(tc.manual_schedule())
         const = ctx.enter_context(tc.tile_pool(name="const", bufs=1))
-        loads = ctx.enter_context(tc.tile_pool(name="loads", bufs=NG))
+        loads = ctx.enter_context(tc.tile_pool(name="loads", bufs=1))
         work = ctx.enter_context(tc.tile_pool(name="work", bufs=3))
         quant = ctx.enter_context(tc.tile_pool(name="quant", bufs=2))
         small = ctx.enter_context(tc.tile_pool(name="small", bufs=3))
-        psum = ctx.enter_context(tc.psum_pool(name="psum", bufs=2))
-
-        a0_rows = taylor_a_0.rearrange("u s i o -> (u s i) o")
-        x_in = []
-        w_in = []
-        z_in = []
-        for g in range(NG):
-            s0 = g * G
-            xs = loads.tile([P, G * I], BF16)
-            nc.sync.dma_start(out=xs[:], in_=x[:, s0:s0 + G, :].rearrange("b s i -> b (s i)"))
-            ws = loads.tile([P, G, PACK * NPOW * O], BF16)
-            nc.sync.dma_start(
-                out=ws[:],
-                in_=taylor_a_0_1[0, s0:s0 + G].rearrange("s (p j) w o -> p s (j w o)", j=PACK),
-            )
-            zs = loads.tile([P, ROWS * O], BF16)
-            nc.sync.dma_start(
-                out=zs[:],
-                in_=a0_rows[s0 * I:(s0 + G) * I, :].rearrange("(p r) o -> p (r o)", r=ROWS),
-            )
-            x_in.append(xs)
-            w_in.append(ws)
-            z_in.append(zs)
+        psum = ctx.enter_context(tc.psum_pool(name="psum", bufs=1))
 
         ident = const.tile([P, P], F32)
         make_identity(nc, ident[:])
@@ -68,84 +75,150 @@ def tile_modelsingle_kernel(tc, x, taylor_a_0_1, taylor_a_0, out):
         )
         sel = const.tile([P, G], BF16)
         nc.vector.tensor_copy(out=sel[:], in_=sel_f[:])
+        res = const.tile([P, S * O], F32)
 
-        grouped = {}
+        a0_rows = taylor_a_0.rearrange("u s i o -> (u s i) o")
+        x_in = {}
+        w_in = {}
+        z_in = {}
+
+        def load_x(j):
+            s0, n = xch[j]
+            xs = loads.tile([P, n * I], BF16, name="xs%d" % j)
+            nc.sync.dma_start(out=xs[:], in_=x[:, s0:s0 + n, :].rearrange("b s i -> b (s i)"))
+            x_in[j] = xs
+
+        def load_w(k):
+            s0, n = wch[k]
+            ws = loads.tile([P, n, PACK * NPOW * O], BF16, name="ws%d" % k)
+            nc.sync.dma_start(
+                out=ws[:],
+                in_=taylor_a_0_1[0, s0:s0 + n].rearrange("s (p j) w o -> p s (j w o)", j=PACK),
+            )
+            w_in[k] = ws
+
+        def load_z(z):
+            zs = loads.tile([P, ROWS * O], BF16, name="zs%d" % z)
+            nc.sync.dma_start(
+                out=zs[:],
+                in_=a0_rows[z * G * I:(z + 1) * G * I, :].rearrange("(p r) o -> p (r o)", r=ROWS),
+            )
+            z_in[z] = zs
+
+        for kind, n in (("x", 0), ("w", 0), ("x", 1), ("w", 1), ("x", 2), ("w", 2), ("z", 0), ("w", 3), ("z", 1),
+                        ("x", 3), ("w", 4), ("z", 2), ("x", 4), ("w", 5), ("z", 3), ("x", 5), ("w", 6), ("z", 4),
+                        ("x", 6), ("w", 7), ("z", 5), ("x", 7), ("w", 8), ("z", 6), ("x", 8), ("z", 7),
+                        ("w", 9), ("w", 10), ("w", 11)):
+            if kind == "x":
+                load_x(n)
+            elif kind == "w":
+                load_w(n)
+            else:
+                load_z(n)
+
+        xts = {}
+        xgs = {}
+        ags = {}
+        xqs = {}
+        aqs = {}
+        accs = {}
+        bsums = {}
+        bcols = {}
+        bbs = {}
         biases = {}
 
-        def prepare(g):
-            xw = x_in[g][:].bitcast(F32).rearrange("b (s p u) -> b s u p", s=G, u=2)
-            xg = work.tile([P, NPOW * G * B * PACK], BF16, align_bytes=64)
-            xg_words = xg[:].bitcast(F32).rearrange(
-                "p (w h c u) -> p w h c u", w=NPOW, h=G // 2, u=2
-            )
-            xg_vals = xg[:].rearrange(
-                "p (w h c u e) -> p w h c u e", w=NPOW, h=G // 2, u=2, e=2
-            )
-            for h in range(G // 2):
-                xt = psum.tile([P, 4 * B], F32, tag="xt")
+        def transposes(j):
+            s0, n = xch[j]
+            xw = x_in[j][:].bitcast(F32).rearrange("b (s p u) -> b s u p", s=n, u=2)
+            banks = []
+            for h in range(n // 2):
+                xt = psum.tile([P, 4 * B], F32, tag="xt", bufs=4, name="xt")
                 for u in range(2):
                     for sl in range(2):
                         col = (u * 2 + sl) * B
                         nc.tensor.transpose(
                             out=xt[:, col:col + B], in_=xw[:, 2 * h + sl, u, :], identity=ident[:]
                         )
-                nc.scalar.copy(
-                    out=xg_words[:, 0, h], in_=xt[:].rearrange("p (u c) -> p c u", u=2)
-                )
+                banks.append(xt)
+            xts[j] = banks
+
+        def powers(j):
+            s0, n = xch[j]
+            xg = work.tile([P, NPOW * G * B * PACK], BF16, align_bytes=64, name="xg")
+            used = xg[:, 0:NPOW * n * B * PACK]
+            words = used.bitcast(F32).rearrange("p (w h c u) -> p w h c u", w=NPOW, h=n // 2, u=2)
+            vals = used.rearrange("p (w h c u e) -> p w h c u e", w=NPOW, h=n // 2, u=2, e=2)
+            for h in range(n // 2):
+                xt = xts[j][h]
+                nc.scalar.copy(out=words[:, 0, h], in_=xt[:].rearrange("p (u c) -> p c u", u=2))
                 nc.scalar.activation(
-                    out=xg_vals[:, 1, h],
+                    out=vals[:, 1, h],
                     in_=xt[:].bitcast(BF16).rearrange("p (u c e) -> p c u e", u=2, e=2),
                     func=SQUARE,
                 )
+            xgs[j] = xg
 
-            ag = work.tile([P, G * NPOW * O * PACK], BF16, align_bytes=64)
-            src = w_in[g][:].rearrange("p s (t c i) -> p s c t i", t=PACK, i=4)
-            dst = ag[:].rearrange("p (s c i t) -> p s c t i", s=G, i=4, t=PACK)
-            nc.vector.tensor_copy(out=dst[:, 0:2], in_=src[:, 0:2])
-            if g in SCALAR_GROUPS:
-                nc.vector.tensor_copy(out=dst[:, 2], in_=src[:, 2])
-                nc.scalar.copy(out=dst[:, 3], in_=src[:, 3])
-            else:
-                nc.vector.tensor_copy(out=dst[:, 2:4], in_=src[:, 2:4])
-            grouped[g] = (xg, ag)
-
-            bsum = psum.tile([P, G], F32, tag="bsum", bufs=1)
-            for r in range(ROWS):
-                nc.tensor.matmul(
-                    out=bsum[:],
-                    lhsT=z_in[g][:, r * O:(r + 1) * O],
-                    rhs=sel[:],
-                    start=(r == 0),
-                    stop=(r == ROWS - 1),
+        def regroup(k):
+            s0, n = wch[k]
+            ag = work.tile([P, G * NPOW * O * PACK], BF16, align_bytes=64, name="ag")
+            src = w_in[k][:].rearrange("p s (t c i) -> p s c t i", t=PACK, i=4)
+            dst = ag[:, 0:n * NPOW * O * PACK].rearrange(
+                "p (s c i t) -> p s c t i", s=n, i=4, t=PACK
+            )
+            mine = [sl for sl in range(n) if s0 + sl not in SCALAR_S]
+            if len(mine) == 1:
+                nc.vector.tensor_copy(out=dst[:, mine[0]], in_=src[:, mine[0]])
+            elif len(mine) > 1:
+                nc.vector.tensor_copy(
+                    out=dst[:, mine[0]:mine[-1] + 1], in_=src[:, mine[0]:mine[-1] + 1]
                 )
-            bcol = small.tile([P, G], F32)
-            nc.scalar.copy(out=bcol[:], in_=bsum[:])
-            bb = psum.tile([P, G * O], F32, tag="bb")
-            for c in range(G):
-                nc.tensor.transpose(
-                    out=bb[:, c * O:(c + 1) * O],
-                    in_=bcol[:, c:c + 1].to_broadcast([P, P]),
-                    identity=ident[:],
-                )
-            bias = small.tile([P, G * O], F32)
-            nc.scalar.copy(out=bias[:], in_=bb[:])
-            biases[g] = bias
+            for sl in range(n):
+                if s0 + sl in SCALAR_S:
+                    nc.scalar.copy(out=dst[:, sl], in_=src[:, sl])
+            ags[k] = ag
 
-        def multiply(g):
-            xg, ag = grouped[g]
-            a_codes = quant.tile([P, G * NPOW * O], U32, align_bytes=64)
-            a_scales = quant.tile([P, G * NPOW * O], U8, align_bytes=64)
-            nc.vector.quantize_mx(out=a_codes[:].bitcast(FP8X4), scales=a_scales[:], in_=ag[:])
-            x_codes = quant.tile([P, NPOW * G * B], U32, align_bytes=64)
-            x_scales = quant.tile([P, NPOW * G * B], U8, align_bytes=64)
-            nc.vector.quantize_mx(out=x_codes[:].bitcast(FP8X4), scales=x_scales[:], in_=xg[:])
-            acc = psum.tile([P, G * O], F32, tag="acc")
-            for s in range(G):
+        def quantise_w(k):
+            s0, n = wch[k]
+            cols = n * NPOW * O
+            codes = quant.tile([P, G * NPOW * O], U32, align_bytes=64, name="a_codes")
+            scales = quant.tile([P, G * NPOW * O], U8, align_bytes=64, name="a_scales")
+            nc.vector.quantize_mx(
+                out=codes[:, 0:cols].bitcast(FP8X4),
+                scales=scales[:, 0:cols],
+                in_=ags[k][:, 0:cols * PACK],
+            )
+            aqs[k] = (codes, scales)
+
+        def quantise_x(j):
+            s0, n = xch[j]
+            cols = NPOW * n * B
+            codes = quant.tile([P, NPOW * G * B], U32, align_bytes=64, name="x_codes")
+            scales = quant.tile([P, NPOW * G * B], U8, align_bytes=64, name="x_scales")
+            nc.vector.quantize_mx(
+                out=codes[:, 0:cols].bitcast(FP8X4),
+                scales=scales[:, 0:cols],
+                in_=xgs[j][:, 0:cols * PACK],
+            )
+            xqs[j] = (codes, scales)
+
+        def multiply(k):
+            s0, n = wch[k]
+            z = s0 // G
+            if z not in accs:
+                acc_new = psum.tile([P, G * O], F32, tag="acc", bufs=2, name="acc")
+                accs[z] = acc_new
+            acc = accs[z]
+            a_codes, a_scales = aqs[k]
+            for sl in range(n):
+                s = s0 + sl
+                j, xl, xn = x_of_s[s]
+                x_codes, x_scales = xqs[j]
+                oc = (s - z * G) * O
                 for w in range(NPOW):
-                    xc = (w * G + s) * B
-                    ac = (s * NPOW + w) * O
+                    xc = (w * xn + xl) * B
+                    ac = (sl * NPOW + w) * O
                     nc.tensor.matmul_mx(
-                        out=acc[:, s * O:(s + 1) * O],
+                        out=acc[:, oc:oc + O],
                         lhsT=x_codes[:, xc:xc + B].bitcast(FP8X4),
                         lhsT_scale=x_scales[:, xc:xc + B],
                         rhs=a_codes[:, ac:ac + O].bitcast(FP8X4),
@@ -153,14 +226,74 @@ def tile_modelsingle_kernel(tc, x, taylor_a_0_1, taylor_a_0, out):
                         start=(w == 0),
                         stop=(w == NPOW - 1),
                     )
-            res = small.tile([P, G * O], F32)
-            nc.vector.tensor_tensor(out=res[:], in0=acc[:], in1=biases[g][:], op=ADD)
+
+        def finish(c):
+            s0, n = wch[c]
+            z = s0 // G
+            lo = (s0 - z * G) * O
+            nc.vector.tensor_tensor(
+                out=res[:, s0 * O:(s0 + n) * O],
+                in0=accs[z][:, lo:lo + n * O],
+                in1=biases[z][:, lo:lo + n * O],
+                op=ADD,
+            )
             nc.sync.dma_start(
-                out=out[:, g * G:(g + 1) * G, :].rearrange("b s o -> b (s o)"), in_=res[:]
+                out=out[:, s0:s0 + n, :].rearrange("b s o -> b (s o)"),
+                in_=res[:, s0 * O:(s0 + n) * O],
             )
 
-        prepare(0)
-        for g in range(1, NG):
-            prepare(g)
-            multiply(g - 1)
-        multiply(NG - 1)
+        def bias_sums(z):
+            bsum = psum.tile([P, G], F32, tag="bsum", name="bsum")
+            for r in range(ROWS):
+                nc.tensor.matmul(
+                    out=bsum[:],
+                    lhsT=z_in[z][:, r * O:(r + 1) * O],
+                    rhs=sel[:],
+                    start=(r == 0),
+                    stop=(r == ROWS - 1),
+                )
+            bsums[z] = bsum
+
+        def bias_column(z):
+            bcol = small.tile([P, G], F32, name="bcol")
+            nc.scalar.copy(out=bcol[:], in_=bsums[z][:])
+            bcols[z] = bcol
+
+        def bias_spread(z):
+            bb = psum.tile([P, G * O], F32, tag="bb", name="bb")
+            for c in range(G):
+                nc.tensor.transpose(
+                    out=bb[:, c * O:(c + 1) * O],
+                    in_=bcols[z][:, c:c + 1].to_broadcast([P, P]),
+                    identity=ident[:],
+                )
+            bbs[z] = bb
+
+        def bias_out(z):
+            bias = small.tile([P, G * O], F32, name="bias")
+            nc.scalar.copy(out=bias[:], in_=bbs[z][:])
+            biases[z] = bias
+
+        for k in range(-2, nw + 2):
+            z = zit.get(k)
+            if k + 2 in x_tied:
+                transposes(x_tied[k + 2])
+            if z is not None:
+                bias_sums(z)
+            if k + 1 in x_tied:
+                powers(x_tied[k + 1])
+            if z is not None:
+                bias_column(z)
+            if 0 <= k + 1 < nw:
+                regroup(k + 1)
+            if z is not None:
+                bias_spread(z)
+            if 0 <= k < nw:
+                quantise_w(k)
+                if k in x_tied:
+                    quantise_x(x_tied[k])
+                multiply(k)
+            if z is not None:
+                bias_out(z)
+            for c in dit.get(k, []):
+                finish(c)

@@ -26,9 +26,40 @@ ROWS = G * I // P
 FLOPS = 2 * B * S * NPOW * I * O
 
 MANUAL = True
-W_SIZES = (2, 2, 2, 2, 4, 4, 4, 4, 4, 2, 1, 1)
+W_SIZES = (2, 2, 4, 4, 4, 4, 4, 4, 2, 1, 1)
 X_SIZES = (2, 2, 4, 4, 4, 4, 4, 4, 4)
-SCALAR_S = (11, 15, 19, 23, 27, 31)
+SCALAR_S = (23, 30, 31,)
+XT_BANKS = 4
+LOADS = (
+    ("x", 0), ("w", 0), ("x", 1), ("w", 1), ("x", 2), ("w", 2), ("z", 0), ("x", 3), ("w", 3), ("z", 1),
+    ("x", 4), ("w", 4), ("z", 2), ("x", 5), ("w", 5), ("z", 3), ("x", 6), ("w", 6), ("z", 4), ("x", 7),
+    ("w", 7), ("z", 5), ("x", 8), ("z", 6), ("z", 7), ("w", 8), ("w", 9), ("w", 10),
+)
+PROGRAM = (
+    ("T", 0, 0), ("EV", 0, 0), ("R", 0, 0), ("SQ", 0, 0), ("T", 1, 0), ("QA", 0, 0),
+    ("EV", 1, 0), ("R", 1, 0), ("SQ", 1, 0), ("T", 2, 0), ("QX", 0, 0), ("T", 2, 1),
+    ("QA", 1, 0), ("EV", 2, 0), ("QX", 1, 0), ("M", 0, 0), ("SQ", 2, 0), ("M", 1, 0),
+    ("R", 2, 0), ("EV", 2, 1), ("SQ", 2, 1), ("Z1", 0, 0), ("QA", 2, 0), ("T", 3, 0),
+    ("Z2", 0, 0), ("Z3", 0, 0), ("EV", 3, 0), ("T", 3, 1), ("QX", 2, 0), ("Z4", 0, 0),
+    ("SQ", 3, 0), ("R", 3, 0), ("EV", 3, 1), ("Z1", 1, 0), ("SQ", 3, 1), ("D", 0, 0),
+    ("T", 4, 0), ("D", 1, 0), ("Z2", 1, 0), ("T", 4, 1), ("QA", 3, 0), ("EV", 4, 0),
+    ("M", 2, 0), ("SQ", 4, 0), ("QX", 3, 0), ("Z3", 1, 0), ("EV", 4, 1), ("R", 4, 0),
+    ("Z4", 1, 0), ("M", 3, 0), ("SQ", 4, 1), ("Z1", 2, 0), ("D", 2, 0), ("T", 5, 0),
+    ("Z2", 2, 0), ("T", 5, 1), ("QA", 4, 0), ("EV", 5, 0), ("Z3", 2, 0), ("SQ", 5, 0),
+    ("QX", 4, 0), ("Z4", 2, 0), ("R", 5, 0), ("Z1", 3, 0), ("EV", 5, 1), ("M", 4, 0),
+    ("SQ", 5, 1), ("T", 6, 0), ("Z2", 3, 0), ("D", 3, 0), ("T", 6, 1), ("QA", 5, 0),
+    ("EV", 6, 0), ("Z3", 3, 0), ("SQ", 6, 0), ("QX", 5, 0), ("Z4", 3, 0), ("Z1", 4, 0),
+    ("R", 6, 0), ("EV", 6, 1), ("M", 5, 0), ("SQ", 6, 1), ("T", 7, 0), ("D", 4, 0),
+    ("Z2", 4, 0), ("Rs", 6, 0), ("T", 7, 1), ("QX", 6, 0), ("Z3", 4, 0), ("EV", 7, 0),
+    ("QA", 6, 0), ("SQ", 7, 0), ("Z1", 5, 0), ("R", 7, 0), ("Z4", 4, 0), ("M", 6, 0),
+    ("EV", 7, 1), ("Z2", 5, 0), ("SQ", 7, 1), ("T", 8, 0), ("Z3", 5, 0), ("D", 5, 0),
+    ("EV", 8, 0), ("Z1", 6, 0), ("QA", 7, 0), ("Z4", 5, 0), ("T", 8, 1), ("SQ", 8, 0),
+    ("QX", 7, 0), ("Z2", 6, 0), ("EV", 8, 1), ("D", 6, 0), ("Z3", 6, 0), ("SQ", 8, 1),
+    ("R", 8, 0), ("M", 7, 0), ("Z4", 6, 0), ("QA", 8, 0), ("Z1", 7, 0), ("Rs", 9, 0),
+    ("QX", 8, 0), ("Z2", 7, 0), ("Rs", 10, 0), ("D", 7, 0), ("Z3", 7, 0), ("QA", 9, 0),
+    ("M", 8, 0), ("Z4", 7, 0), ("M", 9, 0), ("QA", 10, 0), ("D", 8, 0), ("D", 9, 0),
+    ("M", 10, 0), ("D", 10, 0),
+)
 
 
 def starts(sizes):
@@ -44,18 +75,10 @@ def tile_modelsingle_kernel(tc, x, taylor_a_0_1, taylor_a_0, out):
     nc = tc.nc
     wch = starts(W_SIZES)
     xch = starts(X_SIZES)
-    nw = len(wch)
-    w_at = dict((s0, k) for k, (s0, n) in enumerate(wch))
-    x_tied = dict((w_at[s0], j) for j, (s0, n) in enumerate(xch))
     x_of_s = {}
     for j, (s0, n) in enumerate(xch):
         for sl in range(n):
             x_of_s[s0 + sl] = (j, sl, n)
-    zit = dict((z + 2, z) for z in range(NG))
-    dit = {}
-    for c, (s0, n) in enumerate(wch):
-        k = max(c + 1, s0 // G + 3)
-        dit[k] = dit.get(k, []) + [c]
 
     with ExitStack() as ctx:
         if MANUAL:
@@ -81,40 +104,29 @@ def tile_modelsingle_kernel(tc, x, taylor_a_0_1, taylor_a_0, out):
         x_in = {}
         w_in = {}
         z_in = {}
-
-        def load_x(j):
-            s0, n = xch[j]
-            xs = loads.tile([P, n * I], BF16, name="xs%d" % j)
-            nc.sync.dma_start(out=xs[:], in_=x[:, s0:s0 + n, :].rearrange("b s i -> b (s i)"))
-            x_in[j] = xs
-
-        def load_w(k):
-            s0, n = wch[k]
-            ws = loads.tile([P, n, PACK * NPOW * O], BF16, name="ws%d" % k)
-            nc.sync.dma_start(
-                out=ws[:],
-                in_=taylor_a_0_1[0, s0:s0 + n].rearrange("s (p j) w o -> p s (j w o)", j=PACK),
-            )
-            w_in[k] = ws
-
-        def load_z(z):
-            zs = loads.tile([P, ROWS * O], BF16, name="zs%d" % z)
-            nc.sync.dma_start(
-                out=zs[:],
-                in_=a0_rows[z * G * I:(z + 1) * G * I, :].rearrange("(p r) o -> p (r o)", r=ROWS),
-            )
-            z_in[z] = zs
-
-        for kind, n in (("x", 0), ("w", 0), ("x", 1), ("w", 1), ("x", 2), ("w", 2), ("z", 0), ("w", 3), ("z", 1),
-                        ("x", 3), ("w", 4), ("z", 2), ("x", 4), ("w", 5), ("z", 3), ("x", 5), ("w", 6), ("z", 4),
-                        ("x", 6), ("w", 7), ("z", 5), ("x", 7), ("w", 8), ("z", 6), ("x", 8), ("z", 7),
-                        ("w", 9), ("w", 10), ("w", 11)):
+        for kind, n_ld in LOADS:
             if kind == "x":
-                load_x(n)
+                s0, n = xch[n_ld]
+                xs = loads.tile([P, n * I], BF16, name="xs%d" % n_ld)
+                nc.sync.dma_start(out=xs[:], in_=x[:, s0:s0 + n, :].rearrange("b s i -> b (s i)"))
+                x_in[n_ld] = xs
             elif kind == "w":
-                load_w(n)
+                s0, n = wch[n_ld]
+                ws = loads.tile([P, n, PACK * NPOW * O], BF16, name="ws%d" % n_ld)
+                nc.sync.dma_start(
+                    out=ws[:],
+                    in_=taylor_a_0_1[0, s0:s0 + n].rearrange("s (p j) w o -> p s (j w o)", j=PACK),
+                )
+                w_in[n_ld] = ws
             else:
-                load_z(n)
+                zs = loads.tile([P, ROWS * O], BF16, name="zs%d" % n_ld)
+                nc.sync.dma_start(
+                    out=zs[:],
+                    in_=a0_rows[n_ld * G * I:(n_ld + 1) * G * I, :].rearrange(
+                        "(p r) o -> p (r o)", r=ROWS
+                    ),
+                )
+                z_in[n_ld] = zs
 
         xts = {}
         xgs = {}
@@ -127,55 +139,69 @@ def tile_modelsingle_kernel(tc, x, taylor_a_0_1, taylor_a_0, out):
         bbs = {}
         biases = {}
 
-        def transposes(j):
+        def transposes(j, h):
             s0, n = xch[j]
             xw = x_in[j][:].bitcast(F32).rearrange("b (s p u) -> b s u p", s=n, u=2)
-            banks = []
-            for h in range(n // 2):
-                xt = psum.tile([P, 4 * B], F32, tag="xt", bufs=4, name="xt")
-                for u in range(2):
-                    for sl in range(2):
-                        col = (u * 2 + sl) * B
-                        nc.tensor.transpose(
-                            out=xt[:, col:col + B], in_=xw[:, 2 * h + sl, u, :], identity=ident[:]
-                        )
-                banks.append(xt)
-            xts[j] = banks
+            xt = psum.tile([P, 4 * B], F32, tag="xt", bufs=XT_BANKS, name="xt")
+            for u in range(2):
+                for sl in range(2):
+                    col = (u * 2 + sl) * B
+                    nc.tensor.transpose(
+                        out=xt[:, col:col + B], in_=xw[:, 2 * h + sl, u, :], identity=ident[:]
+                    )
+            xts[(j, h)] = xt
 
-        def powers(j):
+        def x_tile(j):
+            if j not in xgs:
+                xg_new = work.tile([P, NPOW * G * B * PACK], BF16, align_bytes=64, name="xg")
+                xgs[j] = xg_new
             s0, n = xch[j]
-            xg = work.tile([P, NPOW * G * B * PACK], BF16, align_bytes=64, name="xg")
-            used = xg[:, 0:NPOW * n * B * PACK]
-            words = used.bitcast(F32).rearrange("p (w h c u) -> p w h c u", w=NPOW, h=n // 2, u=2)
-            vals = used.rearrange("p (w h c u e) -> p w h c u e", w=NPOW, h=n // 2, u=2, e=2)
-            for h in range(n // 2):
-                xt = xts[j][h]
-                nc.scalar.copy(out=words[:, 0, h], in_=xt[:].rearrange("p (u c) -> p c u", u=2))
-                nc.scalar.activation(
-                    out=vals[:, 1, h],
-                    in_=xt[:].bitcast(BF16).rearrange("p (u c e) -> p c u e", u=2, e=2),
-                    func=SQUARE,
-                )
-            xgs[j] = xg
+            return xgs[j][:, 0:NPOW * n * B * PACK], n
 
-        def regroup(k):
+        def first_power(j, h):
+            used, n = x_tile(j)
+            words = used.bitcast(F32).rearrange("p (w h c u) -> p w h c u", w=NPOW, h=n // 2, u=2)
+            nc.scalar.copy(
+                out=words[:, 0, h], in_=xts[(j, h)][:].rearrange("p (u c) -> p c u", u=2)
+            )
+
+        def second_power(j, h):
+            used, n = x_tile(j)
+            vals = used.rearrange("p (w h c u e) -> p w h c u e", w=NPOW, h=n // 2, u=2, e=2)
+            nc.scalar.activation(
+                out=vals[:, 1, h],
+                in_=xts[(j, h)][:].bitcast(BF16).rearrange("p (u c e) -> p c u e", u=2, e=2),
+                func=SQUARE,
+            )
+
+        def w_views(k):
             s0, n = wch[k]
-            ag = work.tile([P, G * NPOW * O * PACK], BF16, align_bytes=64, name="ag")
+            if k not in ags:
+                ag_new = work.tile([P, G * NPOW * O * PACK], BF16, align_bytes=64, name="ag")
+                ags[k] = ag_new
             src = w_in[k][:].rearrange("p s (t c i) -> p s c t i", t=PACK, i=4)
-            dst = ag[:, 0:n * NPOW * O * PACK].rearrange(
+            dst = ags[k][:, 0:n * NPOW * O * PACK].rearrange(
                 "p (s c i t) -> p s c t i", s=n, i=4, t=PACK
             )
+            return src, dst
+
+        def regroup_vector(k):
+            s0, n = wch[k]
+            src, dst = w_views(k)
             mine = [sl for sl in range(n) if s0 + sl not in SCALAR_S]
             if len(mine) == 1:
                 nc.vector.tensor_copy(out=dst[:, mine[0]], in_=src[:, mine[0]])
-            elif len(mine) > 1:
+            else:
                 nc.vector.tensor_copy(
                     out=dst[:, mine[0]:mine[-1] + 1], in_=src[:, mine[0]:mine[-1] + 1]
                 )
+
+        def regroup_scalar(k):
+            s0, n = wch[k]
+            src, dst = w_views(k)
             for sl in range(n):
                 if s0 + sl in SCALAR_S:
                     nc.scalar.copy(out=dst[:, sl], in_=src[:, sl])
-            ags[k] = ag
 
         def quantise_w(k):
             s0, n = wch[k]
@@ -203,17 +229,14 @@ def tile_modelsingle_kernel(tc, x, taylor_a_0_1, taylor_a_0, out):
 
         def multiply(k):
             s0, n = wch[k]
-            z = s0 // G
-            if z not in accs:
-                acc_new = psum.tile([P, G * O], F32, tag="acc", bufs=2, name="acc")
-                accs[z] = acc_new
-            acc = accs[z]
+            acc = psum.tile([P, G * O], F32, tag="acc", bufs=2, name="acc")
+            accs[k] = acc
             a_codes, a_scales = aqs[k]
             for sl in range(n):
                 s = s0 + sl
                 j, xl, xn = x_of_s[s]
                 x_codes, x_scales = xqs[j]
-                oc = (s - z * G) * O
+                oc = sl * O
                 for w in range(NPOW):
                     xc = (w * xn + xl) * B
                     ac = (sl * NPOW + w) * O
@@ -233,7 +256,7 @@ def tile_modelsingle_kernel(tc, x, taylor_a_0_1, taylor_a_0, out):
             lo = (s0 - z * G) * O
             nc.vector.tensor_tensor(
                 out=res[:, s0 * O:(s0 + n) * O],
-                in0=accs[z][:, lo:lo + n * O],
+                in0=accs[c][:, 0:n * O],
                 in1=biases[z][:, lo:lo + n * O],
                 op=ADD,
             )
@@ -274,26 +297,30 @@ def tile_modelsingle_kernel(tc, x, taylor_a_0_1, taylor_a_0, out):
             nc.scalar.copy(out=bias[:], in_=bbs[z][:])
             biases[z] = bias
 
-        for k in range(-2, nw + 2):
-            z = zit.get(k)
-            if k + 2 in x_tied:
-                transposes(x_tied[k + 2])
-            if z is not None:
-                bias_sums(z)
-            if k + 1 in x_tied:
-                powers(x_tied[k + 1])
-            if z is not None:
-                bias_column(z)
-            if 0 <= k + 1 < nw:
-                regroup(k + 1)
-            if z is not None:
-                bias_spread(z)
-            if 0 <= k < nw:
-                quantise_w(k)
-                if k in x_tied:
-                    quantise_x(x_tied[k])
-                multiply(k)
-            if z is not None:
-                bias_out(z)
-            for c in dit.get(k, []):
-                finish(c)
+        for op, a, h in PROGRAM:
+            if op == "T":
+                transposes(a, h)
+            elif op == "EV":
+                first_power(a, h)
+            elif op == "SQ":
+                second_power(a, h)
+            elif op == "R":
+                regroup_vector(a)
+            elif op == "Rs":
+                regroup_scalar(a)
+            elif op == "QA":
+                quantise_w(a)
+            elif op == "QX":
+                quantise_x(a)
+            elif op == "M":
+                multiply(a)
+            elif op == "D":
+                finish(a)
+            elif op == "Z1":
+                bias_sums(a)
+            elif op == "Z2":
+                bias_column(a)
+            elif op == "Z3":
+                bias_spread(a)
+            else:
+                bias_out(a)

@@ -16,73 +16,49 @@ P = 128
 B = 128
 S = 32
 I = 512
-NPOW = 2
+POWERS = 2
 O = 128
 PACK = 4
-G = 4
-NG = S // G
-ROWS = G * I // P
+GROUP = 4
+N_GROUPS = S // GROUP
+ROWS = GROUP * I // P
+PAIR = 2
 
-FLOPS = 2 * B * S * NPOW * I * O
+FLOPS = 2 * B * S * POWERS * I * O
 
-MANUAL = True
-W_SIZES = (2, 2, 4, 4, 4, 4, 4, 4, 2, 1, 1)
-X_SIZES = (2, 2, 4, 4, 4, 4, 4, 4, 4)
-SCALAR_S = (23, 30, 31,)
-XT_BANKS = 4
-LOADS = (
-    ("x", 0), ("w", 0), ("x", 1), ("w", 1), ("x", 2), ("w", 2), ("z", 0), ("x", 3), ("w", 3), ("z", 1),
-    ("x", 4), ("w", 4), ("z", 2), ("x", 5), ("w", 5), ("z", 3), ("x", 6), ("w", 6), ("z", 4), ("x", 7),
-    ("w", 7), ("z", 5), ("x", 8), ("z", 6), ("z", 7), ("w", 8), ("w", 9), ("w", 10),
-)
-PROGRAM = (
-    ("T", 0, 0), ("EV", 0, 0), ("R", 0, 0), ("SQ", 0, 0), ("T", 1, 0), ("QA", 0, 0),
-    ("EV", 1, 0), ("R", 1, 0), ("SQ", 1, 0), ("T", 2, 0), ("QX", 0, 0), ("T", 2, 1),
-    ("QA", 1, 0), ("EV", 2, 0), ("QX", 1, 0), ("M", 0, 0), ("SQ", 2, 0), ("M", 1, 0),
-    ("R", 2, 0), ("EV", 2, 1), ("SQ", 2, 1), ("Z1", 0, 0), ("QA", 2, 0), ("T", 3, 0),
-    ("Z2", 0, 0), ("Z3", 0, 0), ("EV", 3, 0), ("T", 3, 1), ("QX", 2, 0), ("Z4", 0, 0),
-    ("SQ", 3, 0), ("R", 3, 0), ("EV", 3, 1), ("Z1", 1, 0), ("SQ", 3, 1), ("D", 0, 0),
-    ("T", 4, 0), ("D", 1, 0), ("Z2", 1, 0), ("T", 4, 1), ("QA", 3, 0), ("EV", 4, 0),
-    ("M", 2, 0), ("SQ", 4, 0), ("QX", 3, 0), ("Z3", 1, 0), ("EV", 4, 1), ("R", 4, 0),
-    ("Z4", 1, 0), ("M", 3, 0), ("SQ", 4, 1), ("Z1", 2, 0), ("D", 2, 0), ("T", 5, 0),
-    ("Z2", 2, 0), ("T", 5, 1), ("QA", 4, 0), ("EV", 5, 0), ("Z3", 2, 0), ("SQ", 5, 0),
-    ("QX", 4, 0), ("Z4", 2, 0), ("R", 5, 0), ("Z1", 3, 0), ("EV", 5, 1), ("M", 4, 0),
-    ("SQ", 5, 1), ("T", 6, 0), ("Z2", 3, 0), ("D", 3, 0), ("T", 6, 1), ("QA", 5, 0),
-    ("EV", 6, 0), ("Z3", 3, 0), ("SQ", 6, 0), ("QX", 5, 0), ("Z4", 3, 0), ("Z1", 4, 0),
-    ("R", 6, 0), ("EV", 6, 1), ("M", 5, 0), ("SQ", 6, 1), ("T", 7, 0), ("D", 4, 0),
-    ("Z2", 4, 0), ("Rs", 6, 0), ("T", 7, 1), ("QX", 6, 0), ("Z3", 4, 0), ("EV", 7, 0),
-    ("QA", 6, 0), ("SQ", 7, 0), ("Z1", 5, 0), ("R", 7, 0), ("Z4", 4, 0), ("M", 6, 0),
-    ("EV", 7, 1), ("Z2", 5, 0), ("SQ", 7, 1), ("T", 8, 0), ("Z3", 5, 0), ("D", 5, 0),
-    ("EV", 8, 0), ("Z1", 6, 0), ("QA", 7, 0), ("Z4", 5, 0), ("T", 8, 1), ("SQ", 8, 0),
-    ("QX", 7, 0), ("Z2", 6, 0), ("EV", 8, 1), ("D", 6, 0), ("Z3", 6, 0), ("SQ", 8, 1),
-    ("R", 8, 0), ("M", 7, 0), ("Z4", 6, 0), ("QA", 8, 0), ("Z1", 7, 0), ("Rs", 9, 0),
-    ("QX", 8, 0), ("Z2", 7, 0), ("Rs", 10, 0), ("D", 7, 0), ("Z3", 7, 0), ("QA", 9, 0),
-    ("M", 8, 0), ("Z4", 7, 0), ("M", 9, 0), ("QA", 10, 0), ("D", 8, 0), ("D", 9, 0),
-    ("M", 10, 0), ("D", 10, 0),
-)
+W_CHUNKS = (2, 2, 4, 4, 4, 4, 4, 4, 2, 1, 1)
+X_CHUNKS = (2, 2, 4, 4, 4, 4, 4, 4, 4)
+LARGEST = 4
+SCALAR_REGROUPS = (23, 30, 31)
+BIAS_LOAD_LAG = 2
+X_BANKS = 3
+SUM_BANKS = 3
 
 
-def starts(sizes):
-    res = []
-    s0 = 0
+def chunk_list(sizes):
+    chunks = []
+    first = 0
     for n in sizes:
-        res.append((s0, n))
-        s0 += n
-    return res
+        chunks.append((first, n))
+        first += n
+    return chunks
 
 
 def tile_modelsingle_kernel(tc, x, taylor_a_0_1, taylor_a_0, out):
     nc = tc.nc
-    wch = starts(W_SIZES)
-    xch = starts(X_SIZES)
-    x_of_s = {}
-    for j, (s0, n) in enumerate(xch):
-        for sl in range(n):
-            x_of_s[s0 + sl] = (j, sl, n)
+    w_chunks = chunk_list(W_CHUNKS)
+    x_chunks = chunk_list(X_CHUNKS)
+    n_w = len(w_chunks)
+    w_index = dict((first, k) for k, (first, n) in enumerate(w_chunks))
+    x_with = dict((w_index[first], j) for j, (first, n) in enumerate(x_chunks))
+    x_place = {}
+    for j, (first, n) in enumerate(x_chunks):
+        for place in range(n):
+            x_place[first + place] = (j, place, n)
+    last_group_chunk = w_index[S - GROUP]
 
     with ExitStack() as ctx:
-        if MANUAL:
-            ctx.enter_context(tc.manual_schedule())
+        ctx.enter_context(tc.manual_schedule())
         const = ctx.enter_context(tc.tile_pool(name="const", bufs=1))
         loads = ctx.enter_context(tc.tile_pool(name="loads", bufs=1))
         work = ctx.enter_context(tc.tile_pool(name="work", bufs=3))
@@ -92,235 +68,231 @@ def tile_modelsingle_kernel(tc, x, taylor_a_0_1, taylor_a_0, out):
 
         ident = const.tile([P, P], F32)
         make_identity(nc, ident[:])
-        sel_f = const.tile([P, G], F32)
+        which_s_f32 = const.tile([P, GROUP], F32)
         nc.vector.tensor_reduce(
-            out=sel_f[:], in_=ident[:].rearrange("p (c r) -> p c r", c=G), axis=AXIS_X, op=ADD
+            out=which_s_f32[:],
+            in_=ident[:].rearrange("p (c r) -> p c r", c=GROUP),
+            axis=AXIS_X,
+            op=ADD,
         )
-        sel = const.tile([P, G], BF16)
-        nc.vector.tensor_copy(out=sel[:], in_=sel_f[:])
-        res = const.tile([P, S * O], F32)
+        which_s = const.tile([P, GROUP], BF16)
+        nc.vector.tensor_copy(out=which_s[:], in_=which_s_f32[:])
+        result = const.tile([P, S * O], F32)
 
-        a0_rows = taylor_a_0.rearrange("u s i o -> (u s i) o")
         x_in = {}
         w_in = {}
-        z_in = {}
-        for kind, n_ld in LOADS:
-            if kind == "x":
-                s0, n = xch[n_ld]
-                xs = loads.tile([P, n * I], BF16, name="xs%d" % n_ld)
-                nc.sync.dma_start(out=xs[:], in_=x[:, s0:s0 + n, :].rearrange("b s i -> b (s i)"))
-                x_in[n_ld] = xs
-            elif kind == "w":
-                s0, n = wch[n_ld]
-                ws = loads.tile([P, n, PACK * NPOW * O], BF16, name="ws%d" % n_ld)
-                nc.sync.dma_start(
-                    out=ws[:],
-                    in_=taylor_a_0_1[0, s0:s0 + n].rearrange("s (p j) w o -> p s (j w o)", j=PACK),
-                )
-                w_in[n_ld] = ws
-            else:
-                zs = loads.tile([P, ROWS * O], BF16, name="zs%d" % n_ld)
-                nc.sync.dma_start(
-                    out=zs[:],
-                    in_=a0_rows[n_ld * G * I:(n_ld + 1) * G * I, :].rearrange(
-                        "(p r) o -> p (r o)", r=ROWS
-                    ),
-                )
-                z_in[n_ld] = zs
+        a0_in = {}
+        a0_rows = taylor_a_0.rearrange("u s i o -> (u s i) o")
 
-        xts = {}
-        xgs = {}
-        ags = {}
-        xqs = {}
-        aqs = {}
-        accs = {}
-        bsums = {}
-        bcols = {}
-        bbs = {}
-        biases = {}
-
-        def transposes(j, h):
-            s0, n = xch[j]
-            xw = x_in[j][:].bitcast(F32).rearrange("b (s p u) -> b s u p", s=n, u=2)
-            xt = psum.tile([P, 4 * B], F32, tag="xt", bufs=XT_BANKS, name="xt")
-            for u in range(2):
-                for sl in range(2):
-                    col = (u * 2 + sl) * B
-                    nc.tensor.transpose(
-                        out=xt[:, col:col + B], in_=xw[:, 2 * h + sl, u, :], identity=ident[:]
-                    )
-            xts[(j, h)] = xt
-
-        def x_tile(j):
-            if j not in xgs:
-                xg_new = work.tile([P, NPOW * G * B * PACK], BF16, align_bytes=64, name="xg")
-                xgs[j] = xg_new
-            s0, n = xch[j]
-            return xgs[j][:, 0:NPOW * n * B * PACK], n
-
-        def first_power(j, h):
-            used, n = x_tile(j)
-            words = used.bitcast(F32).rearrange("p (w h c u) -> p w h c u", w=NPOW, h=n // 2, u=2)
-            nc.scalar.copy(
-                out=words[:, 0, h], in_=xts[(j, h)][:].rearrange("p (u c) -> p c u", u=2)
+        def load_x(j):
+            first, n = x_chunks[j]
+            x_sb = loads.tile([P, n * I], BF16, name="x_sb%d" % j)
+            nc.sync.dma_start(
+                out=x_sb[:], in_=x[:, first:first + n, :].rearrange("b s i -> b (s i)")
             )
+            x_in[j] = x_sb
 
-        def second_power(j, h):
-            used, n = x_tile(j)
-            vals = used.rearrange("p (w h c u e) -> p w h c u e", w=NPOW, h=n // 2, u=2, e=2)
+        def load_w(k):
+            first, n = w_chunks[k]
+            w_sb = loads.tile([P, n, PACK * POWERS * O], BF16, name="w_sb%d" % k)
+            nc.sync.dma_start(
+                out=w_sb[:],
+                in_=taylor_a_0_1[0, first:first + n].rearrange(
+                    "s (p t) w o -> p s (t w o)", t=PACK
+                ),
+            )
+            w_in[k] = w_sb
+
+        def load_a0(g):
+            a0_sb = loads.tile([P, ROWS * O], BF16, name="a0_sb%d" % g)
+            nc.sync.dma_start(
+                out=a0_sb[:],
+                in_=a0_rows[g * GROUP * I:(g + 1) * GROUP * I, :].rearrange(
+                    "(p r) o -> p (r o)", r=ROWS
+                ),
+            )
+            a0_in[g] = a0_sb
+
+        for k in range(n_w):
+            if k in x_with:
+                load_x(x_with[k])
+            if k == last_group_chunk:
+                for g in range(last_group_chunk - BIAS_LOAD_LAG, N_GROUPS):
+                    load_a0(g)
+            load_w(k)
+            if BIAS_LOAD_LAG <= k < last_group_chunk:
+                load_a0(k - BIAS_LOAD_LAG)
+
+        x_banks = {}
+        x_grouped = {}
+        w_grouped = {}
+        x_quant = {}
+        w_quant = {}
+        sums = {}
+        bias_os = {}
+        bias_column = {}
+        bias_bank = {}
+        bias_sb = {}
+
+        def transpose_x(j):
+            n = x_chunks[j][1]
+            words = x_in[j][:].bitcast(F32).rearrange("b (s p u) -> b s u p", s=n, u=2)
+            for pair in range(n // PAIR):
+                bank = psum.tile([P, 2 * PAIR * B], F32, tag="x_bank", bufs=X_BANKS, name="x_bank")
+                for u in range(2):
+                    for place in range(PAIR):
+                        col = (u * PAIR + place) * B
+                        nc.tensor.transpose(
+                            out=bank[:, col:col + B],
+                            in_=words[:, pair * PAIR + place, u, :],
+                            identity=ident[:],
+                        )
+                x_banks[(j, pair)] = bank
+
+        def powers_of_x(j, pair):
+            n = x_chunks[j][1]
+            if pair == 0:
+                grouped = work.tile([P, POWERS * LARGEST * B * PACK], BF16, align_bytes=64, name="x_grouped")
+                x_grouped[j] = grouped
+            used = x_grouped[j][:, 0:POWERS * n * B * PACK]
+            bank = x_banks[(j, pair)]
+            as_words = used.bitcast(F32).rearrange(
+                "p (w h c u) -> p w h c u", w=POWERS, h=n // PAIR, u=2
+            )
+            nc.scalar.copy(
+                out=as_words[:, 0, pair], in_=bank[:].rearrange("p (u c) -> p c u", u=2)
+            )
+            as_values = used.rearrange(
+                "p (w h c u e) -> p w h c u e", w=POWERS, h=n // PAIR, u=2, e=2
+            )
             nc.scalar.activation(
-                out=vals[:, 1, h],
-                in_=xts[(j, h)][:].bitcast(BF16).rearrange("p (u c e) -> p c u e", u=2, e=2),
+                out=as_values[:, 1, pair],
+                in_=bank[:].bitcast(BF16).rearrange("p (u c e) -> p c u e", u=2, e=2),
                 func=SQUARE,
             )
 
-        def w_views(k):
-            s0, n = wch[k]
-            if k not in ags:
-                ag_new = work.tile([P, G * NPOW * O * PACK], BF16, align_bytes=64, name="ag")
-                ags[k] = ag_new
-            src = w_in[k][:].rearrange("p s (t c i) -> p s c t i", t=PACK, i=4)
-            dst = ags[k][:, 0:n * NPOW * O * PACK].rearrange(
-                "p (s c i t) -> p s c t i", s=n, i=4, t=PACK
+        def regroup_w(k):
+            first, n = w_chunks[k]
+            grouped = work.tile([P, LARGEST * POWERS * O * PACK], BF16, align_bytes=64, name="w_grouped")
+            src = w_in[k][:].rearrange("p s (t c r) -> p s c t r", t=PACK, r=4)
+            dst = grouped[:, 0:n * POWERS * O * PACK].rearrange(
+                "p (s c r t) -> p s c t r", s=n, r=4, t=PACK
             )
-            return src, dst
-
-        def regroup_vector(k):
-            s0, n = wch[k]
-            src, dst = w_views(k)
-            mine = [sl for sl in range(n) if s0 + sl not in SCALAR_S]
+            mine = [place for place in range(n) if first + place not in SCALAR_REGROUPS]
             if len(mine) == 1:
                 nc.vector.tensor_copy(out=dst[:, mine[0]], in_=src[:, mine[0]])
-            else:
+            elif len(mine) > 1:
                 nc.vector.tensor_copy(
                     out=dst[:, mine[0]:mine[-1] + 1], in_=src[:, mine[0]:mine[-1] + 1]
                 )
+            for place in range(n):
+                if first + place in SCALAR_REGROUPS:
+                    nc.scalar.copy(out=dst[:, place], in_=src[:, place])
+            w_grouped[k] = grouped
 
-        def regroup_scalar(k):
-            s0, n = wch[k]
-            src, dst = w_views(k)
-            for sl in range(n):
-                if s0 + sl in SCALAR_S:
-                    nc.scalar.copy(out=dst[:, sl], in_=src[:, sl])
-
-        def quantise_w(k):
-            s0, n = wch[k]
-            cols = n * NPOW * O
-            codes = quant.tile([P, G * NPOW * O], U32, align_bytes=64, name="a_codes")
-            scales = quant.tile([P, G * NPOW * O], U8, align_bytes=64, name="a_scales")
+        def quantise(grouped, columns, name):
+            codes = quant.tile([P, LARGEST * POWERS * O], U32, align_bytes=64, name=name + "_codes")
+            scales = quant.tile([P, LARGEST * POWERS * O], U8, align_bytes=64, name=name + "_scales")
             nc.vector.quantize_mx(
-                out=codes[:, 0:cols].bitcast(FP8X4),
-                scales=scales[:, 0:cols],
-                in_=ags[k][:, 0:cols * PACK],
+                out=codes[:, 0:columns].bitcast(FP8X4),
+                scales=scales[:, 0:columns],
+                in_=grouped[:, 0:columns * PACK],
             )
-            aqs[k] = (codes, scales)
-
-        def quantise_x(j):
-            s0, n = xch[j]
-            cols = NPOW * n * B
-            codes = quant.tile([P, NPOW * G * B], U32, align_bytes=64, name="x_codes")
-            scales = quant.tile([P, NPOW * G * B], U8, align_bytes=64, name="x_scales")
-            nc.vector.quantize_mx(
-                out=codes[:, 0:cols].bitcast(FP8X4),
-                scales=scales[:, 0:cols],
-                in_=xgs[j][:, 0:cols * PACK],
-            )
-            xqs[j] = (codes, scales)
+            return codes, scales
 
         def multiply(k):
-            s0, n = wch[k]
-            acc = psum.tile([P, G * O], F32, tag="acc", bufs=2, name="acc")
-            accs[k] = acc
-            a_codes, a_scales = aqs[k]
-            for sl in range(n):
-                s = s0 + sl
-                j, xl, xn = x_of_s[s]
-                x_codes, x_scales = xqs[j]
-                oc = sl * O
-                for w in range(NPOW):
-                    xc = (w * xn + xl) * B
-                    ac = (sl * NPOW + w) * O
+            first, n = w_chunks[k]
+            bank = psum.tile([P, LARGEST * O], F32, tag="sums", bufs=SUM_BANKS, name="sums")
+            w_codes, w_scales = w_quant[k]
+            for place in range(n):
+                j, x_at, x_n = x_place[first + place]
+                x_codes, x_scales = x_quant[j]
+                for w in range(POWERS):
+                    xc = (w * x_n + x_at) * B
+                    wc = (place * POWERS + w) * O
                     nc.tensor.matmul_mx(
-                        out=acc[:, oc:oc + O],
+                        out=bank[:, place * O:(place + 1) * O],
                         lhsT=x_codes[:, xc:xc + B].bitcast(FP8X4),
                         lhsT_scale=x_scales[:, xc:xc + B],
-                        rhs=a_codes[:, ac:ac + O].bitcast(FP8X4),
-                        rhs_scale=a_scales[:, ac:ac + O],
+                        rhs=w_codes[:, wc:wc + O].bitcast(FP8X4),
+                        rhs_scale=w_scales[:, wc:wc + O],
                         start=(w == 0),
-                        stop=(w == NPOW - 1),
+                        stop=(w == POWERS - 1),
                     )
+            sums[k] = bank
 
-        def finish(c):
-            s0, n = wch[c]
-            z = s0 // G
-            lo = (s0 - z * G) * O
+        def finish(k):
+            first, n = w_chunks[k]
+            g = first // GROUP
+            lo = (first - g * GROUP) * O
             nc.vector.tensor_tensor(
-                out=res[:, s0 * O:(s0 + n) * O],
-                in0=accs[c][:, 0:n * O],
-                in1=biases[z][:, lo:lo + n * O],
+                out=result[:, first * O:(first + n) * O],
+                in0=sums[k][:, 0:n * O],
+                in1=bias_sb[g][:, lo:lo + n * O],
                 op=ADD,
             )
             nc.sync.dma_start(
-                out=out[:, s0:s0 + n, :].rearrange("b s o -> b (s o)"),
-                in_=res[:, s0 * O:(s0 + n) * O],
+                out=out[:, first:first + n, :].rearrange("b s o -> b (s o)"),
+                in_=result[:, first * O:(first + n) * O],
             )
 
-        def bias_sums(z):
-            bsum = psum.tile([P, G], F32, tag="bsum", name="bsum")
+        def sum_a0(g):
+            bank = psum.tile([P, GROUP], F32, tag="bias_os", name="bias_os")
             for r in range(ROWS):
                 nc.tensor.matmul(
-                    out=bsum[:],
-                    lhsT=z_in[z][:, r * O:(r + 1) * O],
-                    rhs=sel[:],
+                    out=bank[:],
+                    lhsT=a0_in[g][:, r * O:(r + 1) * O],
+                    rhs=which_s[:],
                     start=(r == 0),
                     stop=(r == ROWS - 1),
                 )
-            bsums[z] = bsum
+            bias_os[g] = bank
 
-        def bias_column(z):
-            bcol = small.tile([P, G], F32, name="bcol")
-            nc.scalar.copy(out=bcol[:], in_=bsums[z][:])
-            bcols[z] = bcol
+        def bias_to_sbuf(g):
+            column = small.tile([P, GROUP], F32, name="bias_column")
+            nc.scalar.copy(out=column[:], in_=bias_os[g][:])
+            bias_column[g] = column
 
-        def bias_spread(z):
-            bb = psum.tile([P, G * O], F32, tag="bb", name="bb")
-            for c in range(G):
+        def spread_bias(g):
+            bank = psum.tile([P, GROUP * O], F32, tag="bias_bank", name="bias_bank")
+            for c in range(GROUP):
                 nc.tensor.transpose(
-                    out=bb[:, c * O:(c + 1) * O],
-                    in_=bcols[z][:, c:c + 1].to_broadcast([P, P]),
+                    out=bank[:, c * O:(c + 1) * O],
+                    in_=bias_column[g][:, c:c + 1].to_broadcast([P, P]),
                     identity=ident[:],
                 )
-            bbs[z] = bb
+            bias_bank[g] = bank
 
-        def bias_out(z):
-            bias = small.tile([P, G * O], F32, name="bias")
-            nc.scalar.copy(out=bias[:], in_=bbs[z][:])
-            biases[z] = bias
+        def bias_out_of_psum(g):
+            spread = small.tile([P, GROUP * O], F32, name="bias_sb")
+            nc.scalar.copy(out=spread[:], in_=bias_bank[g][:])
+            bias_sb[g] = spread
 
-        for op, a, h in PROGRAM:
-            if op == "T":
-                transposes(a, h)
-            elif op == "EV":
-                first_power(a, h)
-            elif op == "SQ":
-                second_power(a, h)
-            elif op == "R":
-                regroup_vector(a)
-            elif op == "Rs":
-                regroup_scalar(a)
-            elif op == "QA":
-                quantise_w(a)
-            elif op == "QX":
-                quantise_x(a)
-            elif op == "M":
-                multiply(a)
-            elif op == "D":
-                finish(a)
-            elif op == "Z1":
-                bias_sums(a)
-            elif op == "Z2":
-                bias_column(a)
-            elif op == "Z3":
-                bias_spread(a)
-            else:
-                bias_out(a)
+        for k in range(-1, n_w + 2):
+            j_next = x_with.get(k + 1)
+            banks_next = x_chunks[j_next][1] // PAIR if j_next is not None else 0
+            spreading = 0 <= k - 2 < N_GROUPS
+            if j_next is not None:
+                transpose_x(j_next)
+            if spreading:
+                bias_to_sbuf(k - 2)
+                spread_bias(k - 2)
+            if 0 <= k < n_w:
+                w_quant[k] = quantise(w_grouped[k], w_chunks[k][1] * POWERS * O, "w")
+                if k in x_with:
+                    j = x_with[k]
+                    x_quant[j] = quantise(x_grouped[j], x_chunks[j][1] * POWERS * B, "x")
+            if banks_next > 0:
+                powers_of_x(j_next, 0)
+            if 0 <= k + 1 < n_w:
+                regroup_w(k + 1)
+            if spreading:
+                bias_out_of_psum(k - 2)
+            if banks_next > 1:
+                powers_of_x(j_next, 1)
+            if 0 <= k - 2 < n_w:
+                finish(k - 2)
+            if 0 <= k - 1 < N_GROUPS:
+                sum_a0(k - 1)
+            if 0 <= k < n_w:
+                multiply(k)

@@ -29,7 +29,7 @@ FLOPS = 2 * B * S * POWERS * I * O
 W_CHUNKS = (2, 2, 4, 4, 4, 4, 4, 4, 2, 1, 1)
 X_CHUNKS = (2, 2, 4, 4, 4, 4, 4, 4, 4)
 LARGEST = 4
-SCALAR_REGROUPS = (23, 30, 31)
+SCALAR_REGROUPS = (11, 19, 27, 30, 31)
 BIAS_LOAD_LAG = 2
 X_BANKS = 3
 SUM_BANKS = 3

@@ -29,7 +29,7 @@ FLOPS = 2 * B * S * POWERS * I * O
 W_CHUNKS = (2, 2, 4, 4, 4, 4, 4, 4, 2, 1, 1)
 X_CHUNKS = (2, 2, 4, 4, 4, 4, 4, 4, 4)
 LARGEST = 4
-SCALAR_REGROUPS = (11, 19, 27, 30, 31)
+SCALAR_REGROUPS = (30, 31)
 BIAS_LOAD_LAG = 2
 X_BANKS = 3
 SUM_BANKS = 3

@@ -10,6 +10,7 @@ U8 = mybir.dt.uint8
 FP8X4 = mybir.dt.float8_e4m3fn_x4
 ADD = mybir.AluOpType.add
 SQUARE = mybir.ActivationFunctionType.Square
+IDENTITY = mybir.ActivationFunctionType.Identity
 AXIS_X = mybir.AxisListType.X
 
 P = 128
@@ -26,13 +27,19 @@ PAIR = 2
 
 FLOPS = 2 * B * S * POWERS * I * O
 
-W_CHUNKS = (2, 2, 4, 4, 4, 4, 4, 4, 2, 1, 1)
+W_CHUNKS = (2, 2, 4, 4, 4, 4, 4, 4, 2, 2)
 X_CHUNKS = (2, 2, 4, 4, 4, 4, 4, 4, 4)
+OUT_CHUNKS = (4, 4, 4, 4, 4, 4, 4, 2, 1, 1)
 LARGEST = 4
-SCALAR_REGROUPS = (30, 31)
-BIAS_LOAD_LAG = 2
+SUM_LAG = 2
+SUM_CATCH = 4
+A0_BEFORE = 1
+X_AHEAD = 1
+SPLIT = 3
 X_BANKS = 3
-SUM_BANKS = 3
+SUM_BANKS = 2
+OUT_BANKS = 2
+VECTOR_FINISHES = 7
 
 
 def chunk_list(sizes):
@@ -49,13 +56,25 @@ def tile_modelsingle_kernel(tc, x, taylor_a_0_1, taylor_a_0, out):
     w_chunks = chunk_list(W_CHUNKS)
     x_chunks = chunk_list(X_CHUNKS)
     n_w = len(w_chunks)
+    out_chunks = chunk_list(OUT_CHUNKS)
+    n_out = len(out_chunks)
+    out_place = {}
+    for u, (first, n) in enumerate(out_chunks):
+        for place in range(n):
+            out_place[first + place] = (u, place)
     w_index = dict((first, k) for k, (first, n) in enumerate(w_chunks))
     x_with = dict((w_index[first], j) for j, (first, n) in enumerate(x_chunks))
     x_place = {}
     for j, (first, n) in enumerate(x_chunks):
         for place in range(n):
             x_place[first + place] = (j, place, n)
-    last_group_chunk = w_index[S - GROUP]
+    units_at = {}
+    for u, (first, n) in enumerate(out_chunks):
+        k = [i for i, (f, m) in enumerate(w_chunks) if f < first + n <= f + m][0]
+        units_at.setdefault(k, []).append(u)
+    groups_at = {}
+    for g in range(N_GROUPS):
+        groups_at.setdefault(g + SUM_LAG - g // SUM_CATCH, []).append(g)
 
     with ExitStack() as ctx:
         ctx.enter_context(tc.manual_schedule())
@@ -78,6 +97,7 @@ def tile_modelsingle_kernel(tc, x, taylor_a_0_1, taylor_a_0, out):
         which_s = const.tile([P, GROUP], BF16)
         nc.vector.tensor_copy(out=which_s[:], in_=which_s_f32[:])
         result = const.tile([P, S * O], F32)
+        bias = const.tile([P, S], F32)
 
         x_in = {}
         w_in = {}
@@ -92,15 +112,20 @@ def tile_modelsingle_kernel(tc, x, taylor_a_0_1, taylor_a_0, out):
             )
             x_in[j] = x_sb
 
+        def pieces(k):
+            n = w_chunks[k][1]
+            return [(0, n // 2), (n // 2, n)]
+
         def load_w(k):
             first, n = w_chunks[k]
             w_sb = loads.tile([P, n, PACK * POWERS * O], BF16, name="w_sb%d" % k)
-            nc.sync.dma_start(
-                out=w_sb[:],
-                in_=taylor_a_0_1[0, first:first + n].rearrange(
-                    "s (p t) w o -> p s (t w o)", t=PACK
-                ),
-            )
+            for lo, hi in pieces(k) if k < SPLIT or k == n_w - 1 else [(0, n)]:
+                nc.sync.dma_start(
+                    out=w_sb[:, lo:hi],
+                    in_=taylor_a_0_1[0, first + lo:first + hi].rearrange(
+                        "s (p t) w o -> p s (t w o)", t=PACK
+                    ),
+                )
             w_in[k] = w_sb
 
         def load_a0(g):
@@ -116,12 +141,9 @@ def tile_modelsingle_kernel(tc, x, taylor_a_0_1, taylor_a_0, out):
         for k in range(n_w):
             if k in x_with:
                 load_x(x_with[k])
-            if k == last_group_chunk:
-                for g in range(last_group_chunk - BIAS_LOAD_LAG, N_GROUPS):
-                    load_a0(g)
+            for g in groups_at.get(k - A0_BEFORE, ()):
+                load_a0(g)
             load_w(k)
-            if BIAS_LOAD_LAG <= k < last_group_chunk:
-                load_a0(k - BIAS_LOAD_LAG)
 
         x_banks = {}
         x_grouped = {}
@@ -130,9 +152,8 @@ def tile_modelsingle_kernel(tc, x, taylor_a_0_1, taylor_a_0, out):
         w_quant = {}
         sums = {}
         bias_os = {}
-        bias_column = {}
-        bias_bank = {}
-        bias_sb = {}
+        biased_out = {}
+        out_banks = {}
 
         def transpose_x(j):
             n = x_chunks[j][1]
@@ -152,7 +173,7 @@ def tile_modelsingle_kernel(tc, x, taylor_a_0_1, taylor_a_0, out):
         def powers_of_x(j, pair):
             n = x_chunks[j][1]
             if pair == 0:
-                grouped = work.tile([P, POWERS * LARGEST * B * PACK], BF16, align_bytes=64, name="x_grouped")
+                grouped = work.tile([P, POWERS * LARGEST * B * PACK], BF16, align_bytes=64, name="x_grouped", bufs=4)
                 x_grouped[j] = grouped
             used = x_grouped[j][:, 0:POWERS * n * B * PACK]
             bank = x_banks[(j, pair)]
@@ -178,121 +199,121 @@ def tile_modelsingle_kernel(tc, x, taylor_a_0_1, taylor_a_0, out):
             dst = grouped[:, 0:n * POWERS * O * PACK].rearrange(
                 "p (s c r t) -> p s c t r", s=n, r=4, t=PACK
             )
-            mine = [place for place in range(n) if first + place not in SCALAR_REGROUPS]
-            if len(mine) == 1:
-                nc.vector.tensor_copy(out=dst[:, mine[0]], in_=src[:, mine[0]])
-            elif len(mine) > 1:
-                nc.vector.tensor_copy(
-                    out=dst[:, mine[0]:mine[-1] + 1], in_=src[:, mine[0]:mine[-1] + 1]
-                )
-            for place in range(n):
-                if first + place in SCALAR_REGROUPS:
-                    nc.scalar.copy(out=dst[:, place], in_=src[:, place])
+            for lo, hi in pieces(k):
+                nc.vector.tensor_copy(out=dst[:, lo:hi], in_=src[:, lo:hi])
             w_grouped[k] = grouped
 
-        def quantise(grouped, columns, name):
+        def quantise(grouped, windows, name):
             codes = quant.tile([P, LARGEST * POWERS * O], U32, align_bytes=64, name=name + "_codes")
             scales = quant.tile([P, LARGEST * POWERS * O], U8, align_bytes=64, name=name + "_scales")
-            nc.vector.quantize_mx(
-                out=codes[:, 0:columns].bitcast(FP8X4),
-                scales=scales[:, 0:columns],
-                in_=grouped[:, 0:columns * PACK],
-            )
+            for lo, hi in windows:
+                nc.vector.quantize_mx(
+                    out=codes[:, lo:hi].bitcast(FP8X4),
+                    scales=scales[:, lo:hi],
+                    in_=grouped[:, lo * PACK:hi * PACK],
+                )
             return codes, scales
 
         def multiply(k):
             first, n = w_chunks[k]
-            bank = psum.tile([P, LARGEST * O], F32, tag="sums", bufs=SUM_BANKS, name="sums")
             w_codes, w_scales = w_quant[k]
             for place in range(n):
+                u, out_at = out_place[first + place]
+                if out_at == 0:
+                    sums[u] = psum.tile([P, LARGEST * B], F32, tag="sums", bufs=SUM_BANKS, name="sums")
+                bank = sums[u]
                 j, x_at, x_n = x_place[first + place]
                 x_codes, x_scales = x_quant[j]
                 for w in range(POWERS):
                     xc = (w * x_n + x_at) * B
                     wc = (place * POWERS + w) * O
                     nc.tensor.matmul_mx(
-                        out=bank[:, place * O:(place + 1) * O],
-                        lhsT=x_codes[:, xc:xc + B].bitcast(FP8X4),
-                        lhsT_scale=x_scales[:, xc:xc + B],
-                        rhs=w_codes[:, wc:wc + O].bitcast(FP8X4),
-                        rhs_scale=w_scales[:, wc:wc + O],
+                        out=bank[:, out_at * B:(out_at + 1) * B],
+                        lhsT=w_codes[:, wc:wc + O].bitcast(FP8X4),
+                        lhsT_scale=w_scales[:, wc:wc + O],
+                        rhs=x_codes[:, xc:xc + B].bitcast(FP8X4),
+                        rhs_scale=x_scales[:, xc:xc + B],
                         start=(w == 0),
                         stop=(w == POWERS - 1),
                     )
-            sums[k] = bank
 
-        def finish(k):
-            first, n = w_chunks[k]
-            g = first // GROUP
-            lo = (first - g * GROUP) * O
-            nc.vector.tensor_tensor(
-                out=result[:, first * O:(first + n) * O],
-                in0=sums[k][:, 0:n * O],
-                in1=bias_sb[g][:, lo:lo + n * O],
-                op=ADD,
-            )
-            nc.sync.dma_start(
-                out=out[:, first:first + n, :].rearrange("b s o -> b (s o)"),
-                in_=result[:, first * O:(first + n) * O],
-            )
-
-        def sum_a0(g):
-            bank = psum.tile([P, GROUP], F32, tag="bias_os", name="bias_os")
-            for r in range(ROWS):
-                nc.tensor.matmul(
-                    out=bank[:],
-                    lhsT=a0_in[g][:, r * O:(r + 1) * O],
-                    rhs=which_s[:],
-                    start=(r == 0),
-                    stop=(r == ROWS - 1),
+        def add_bias(u):
+            first, n = out_chunks[u]
+            biased = small.tile([P, LARGEST * B], F32, name="biased")
+            for place in range(n):
+                s = first + place
+                nc.scalar.activation(
+                    out=biased[:, place * B:(place + 1) * B],
+                    in_=sums[u][:, place * B:(place + 1) * B],
+                    func=IDENTITY,
+                    bias=bias[:, s:s + 1],
                 )
-            bias_os[g] = bank
+            biased_out[u] = biased
 
-        def bias_to_sbuf(g):
-            column = small.tile([P, GROUP], F32, name="bias_column")
-            nc.scalar.copy(out=column[:], in_=bias_os[g][:])
-            bias_column[g] = column
-
-        def spread_bias(g):
-            bank = psum.tile([P, GROUP * O], F32, tag="bias_bank", name="bias_bank")
-            for c in range(GROUP):
+        def transpose_back(u):
+            n = out_chunks[u][1]
+            bank = psum.tile([P, LARGEST * O], F32, tag="out_bank", bufs=OUT_BANKS, name="out_bank")
+            for place in range(n):
                 nc.tensor.transpose(
-                    out=bank[:, c * O:(c + 1) * O],
-                    in_=bias_column[g][:, c:c + 1].to_broadcast([P, P]),
+                    out=bank[:, place * O:(place + 1) * O],
+                    in_=biased_out[u][:, place * B:(place + 1) * B],
                     identity=ident[:],
                 )
-            bias_bank[g] = bank
+            out_banks[u] = bank
 
-        def bias_out_of_psum(g):
-            spread = small.tile([P, GROUP * O], F32, name="bias_sb")
-            nc.scalar.copy(out=spread[:], in_=bias_bank[g][:])
-            bias_sb[g] = spread
+        def finish(u):
+            first, n = out_chunks[u]
+            dst = result[:, first * O:(first + n) * O]
+            if u < VECTOR_FINISHES:
+                nc.scalar.copy(out=dst, in_=out_banks[u][:, 0:n * O])
+            else:
+                nc.vector.tensor_copy(out=dst, in_=out_banks[u][:, 0:n * O])
+            nc.sync.dma_start(
+                out=out[:, first:first + n, :].rearrange("b s o -> b (s o)"), in_=dst
+            )
 
-        for k in range(-1, n_w + 2):
-            j_next = x_with.get(k + 1)
+        def sum_a0(groups):
+            bank = psum.tile([P, 2 * GROUP], F32, tag="bias_os", name="bias_os")
+            for at, g in enumerate(groups):
+                for r in range(ROWS):
+                    nc.tensor.matmul(
+                        out=bank[:, at * GROUP:(at + 1) * GROUP],
+                        lhsT=a0_in[g][:, r * O:(r + 1) * O],
+                        rhs=which_s[:],
+                        start=(r == 0),
+                        stop=(r == ROWS - 1),
+                    )
+            bias_os[groups[0]] = bank
+
+        def bias_to_sbuf(groups):
+            lo = groups[0] * GROUP
+            n = len(groups) * GROUP
+            nc.scalar.copy(out=bias[:, lo:lo + n], in_=bias_os[groups[0]][:, 0:n])
+
+        for k in range(-X_AHEAD, n_w + 2):
+            j_next = x_with.get(k + X_AHEAD)
             banks_next = x_chunks[j_next][1] // PAIR if j_next is not None else 0
-            spreading = 0 <= k - 2 < N_GROUPS
             if j_next is not None:
                 transpose_x(j_next)
-            if spreading:
-                bias_to_sbuf(k - 2)
-                spread_bias(k - 2)
+            for u in units_at.get(k - 2, ()):
+                transpose_back(u)
             if 0 <= k < n_w:
-                w_quant[k] = quantise(w_grouped[k], w_chunks[k][1] * POWERS * O, "w")
+                w_quant[k] = quantise(w_grouped[k], [(lo * POWERS * O, hi * POWERS * O) for lo, hi in pieces(k)], "w")
                 if k in x_with:
                     j = x_with[k]
-                    x_quant[j] = quantise(x_grouped[j], x_chunks[j][1] * POWERS * B, "x")
+                    x_quant[j] = quantise(x_grouped[j], [(0, x_chunks[j][1] * POWERS * B)], "x")
             if banks_next > 0:
                 powers_of_x(j_next, 0)
             if 0 <= k + 1 < n_w:
                 regroup_w(k + 1)
-            if spreading:
-                bias_out_of_psum(k - 2)
             if banks_next > 1:
                 powers_of_x(j_next, 1)
-            if 0 <= k - 2 < n_w:
-                finish(k - 2)
-            if 0 <= k - 1 < N_GROUPS:
-                sum_a0(k - 1)
+            if k in groups_at:
+                sum_a0(groups_at[k])
+                bias_to_sbuf(groups_at[k])
+            for u in units_at.get(k - 1, ()):
+                add_bias(u)
+            for u in units_at.get(k - 2, ()):
+                finish(u)
             if 0 <= k < n_w:
                 multiply(k)

@@ -31,15 +31,19 @@ W_CHUNKS = (2, 2, 4, 4, 4, 4, 4, 4, 2, 2)
 X_CHUNKS = (2, 2, 4, 4, 4, 4, 4, 4, 4)
 OUT_CHUNKS = (4, 4, 4, 4, 4, 4, 4, 2, 1, 1)
 LARGEST = 4
-SUM_LAG = 2
-SUM_CATCH = 4
-A0_BEFORE = 1
+SUM_STEP = (2, 3, 4, 5, 5, 6, 7, 7)
+A0_LOAD = (3, 4, 5, 6, 6, 7, 8, 8)
+SPREAD_AT = 8
+ADD_POS = 0
+BACK_POS = 0
+SUM_POS = 1
+X0_LATE = False
+FIN_V = (1, 3, 5)
 X_AHEAD = 1
 SPLIT = 3
 X_BANKS = 3
 SUM_BANKS = 2
 OUT_BANKS = 2
-VECTOR_FINISHES = 7
 
 
 def chunk_list(sizes):
@@ -57,7 +61,7 @@ def tile_modelsingle_kernel(tc, x, taylor_a_0_1, taylor_a_0, out):
     x_chunks = chunk_list(X_CHUNKS)
     n_w = len(w_chunks)
     out_chunks = chunk_list(OUT_CHUNKS)
-    n_out = len(out_chunks)
+    direct = [u for u, (first, n) in enumerate(out_chunks) if first >= S - GROUP]
     out_place = {}
     for u, (first, n) in enumerate(out_chunks):
         for place in range(n):
@@ -69,12 +73,15 @@ def tile_modelsingle_kernel(tc, x, taylor_a_0_1, taylor_a_0, out):
         for place in range(n):
             x_place[first + place] = (j, place, n)
     units_at = {}
+    add_at = {}
     for u, (first, n) in enumerate(out_chunks):
         k = [i for i, (f, m) in enumerate(w_chunks) if f < first + n <= f + m][0]
         units_at.setdefault(k, []).append(u)
+        if u not in direct:
+            add_at.setdefault(max(k, SUM_STEP[u]) + 1, []).append(u)
     groups_at = {}
     for g in range(N_GROUPS):
-        groups_at.setdefault(g + SUM_LAG - g // SUM_CATCH, []).append(g)
+        groups_at.setdefault(SUM_STEP[g], []).append(g)
 
     with ExitStack() as ctx:
         ctx.enter_context(tc.manual_schedule())
@@ -98,6 +105,7 @@ def tile_modelsingle_kernel(tc, x, taylor_a_0_1, taylor_a_0, out):
         nc.vector.tensor_copy(out=which_s[:], in_=which_s_f32[:])
         result = const.tile([P, S * O], F32)
         bias = const.tile([P, S], F32)
+        spread = const.tile([P, GROUP * O], F32)
 
         x_in = {}
         w_in = {}
@@ -141,8 +149,9 @@ def tile_modelsingle_kernel(tc, x, taylor_a_0_1, taylor_a_0, out):
         for k in range(n_w):
             if k in x_with:
                 load_x(x_with[k])
-            for g in groups_at.get(k - A0_BEFORE, ()):
-                load_a0(g)
+            for g in range(N_GROUPS):
+                if A0_LOAD[g] == k:
+                    load_a0(g)
             load_w(k)
 
         x_banks = {}
@@ -227,12 +236,15 @@ def tile_modelsingle_kernel(tc, x, taylor_a_0_1, taylor_a_0, out):
                 for w in range(POWERS):
                     xc = (w * x_n + x_at) * B
                     wc = (place * POWERS + w) * O
+                    x_side = (x_codes[:, xc:xc + B].bitcast(FP8X4), x_scales[:, xc:xc + B])
+                    w_side = (w_codes[:, wc:wc + O].bitcast(FP8X4), w_scales[:, wc:wc + O])
+                    stationary, moving = (x_side, w_side) if u in direct else (w_side, x_side)
                     nc.tensor.matmul_mx(
                         out=bank[:, out_at * B:(out_at + 1) * B],
-                        lhsT=w_codes[:, wc:wc + O].bitcast(FP8X4),
-                        lhsT_scale=w_scales[:, wc:wc + O],
-                        rhs=x_codes[:, xc:xc + B].bitcast(FP8X4),
-                        rhs_scale=x_scales[:, xc:xc + B],
+                        lhsT=stationary[0],
+                        lhsT_scale=stationary[1],
+                        rhs=moving[0],
+                        rhs_scale=moving[1],
                         start=(w == 0),
                         stop=(w == POWERS - 1),
                     )
@@ -261,19 +273,52 @@ def tile_modelsingle_kernel(tc, x, taylor_a_0_1, taylor_a_0, out):
                 )
             out_banks[u] = bank
 
-        def finish(u):
+        def store(u):
             first, n = out_chunks[u]
-            dst = result[:, first * O:(first + n) * O]
-            if u < VECTOR_FINISHES:
-                nc.scalar.copy(out=dst, in_=out_banks[u][:, 0:n * O])
-            else:
-                nc.vector.tensor_copy(out=dst, in_=out_banks[u][:, 0:n * O])
             nc.sync.dma_start(
-                out=out[:, first:first + n, :].rearrange("b s o -> b (s o)"), in_=dst
+                out=out[:, first:first + n, :].rearrange("b s o -> b (s o)"),
+                in_=result[:, first * O:(first + n) * O],
             )
 
+        def finish(u):
+            first, n = out_chunks[u]
+            if u in FIN_V:
+                nc.vector.tensor_copy(
+                    out=result[:, first * O:(first + n) * O], in_=out_banks[u][:, 0:n * O]
+                )
+            else:
+                nc.scalar.copy(
+                    out=result[:, first * O:(first + n) * O], in_=out_banks[u][:, 0:n * O]
+                )
+            store(u)
+
+        def spread_bias_t(g):
+            bank = psum.tile([P, LARGEST * O], F32, tag="out_bank", bufs=OUT_BANKS, name="out_bank")
+            for c in range(GROUP):
+                s = g * GROUP + c
+                nc.tensor.transpose(
+                    out=bank[:, c * O:(c + 1) * O],
+                    in_=bias[:, s:s + 1].to_broadcast([P, P]),
+                    identity=ident[:],
+                )
+            out_banks["spread"] = bank
+
+        def spread_bias_s():
+            nc.scalar.copy(out=spread[:], in_=out_banks["spread"][:])
+
+        def finish_direct(u):
+            first, n = out_chunks[u]
+            lo = first * O - (S - GROUP) * O
+            nc.vector.tensor_tensor(
+                out=result[:, first * O:(first + n) * O],
+                in0=sums[u][:, 0:n * O],
+                in1=spread[:, lo:lo + n * O],
+                op=ADD,
+            )
+            store(u)
+
         def sum_a0(groups):
-            bank = psum.tile([P, 2 * GROUP], F32, tag="bias_os", name="bias_os")
+            bank = psum.tile([P, 3 * GROUP], F32, tag="bias_os", name="bias_os")
             for at, g in enumerate(groups):
                 for r in range(ROWS):
                     nc.tensor.matmul(
@@ -286,34 +331,65 @@ def tile_modelsingle_kernel(tc, x, taylor_a_0_1, taylor_a_0, out):
             bias_os[groups[0]] = bank
 
         def bias_to_sbuf(groups):
-            lo = groups[0] * GROUP
-            n = len(groups) * GROUP
-            nc.scalar.copy(out=bias[:, lo:lo + n], in_=bias_os[groups[0]][:, 0:n])
+            for at, g in enumerate(groups):
+                nc.scalar.copy(
+                    out=bias[:, g * GROUP:(g + 1) * GROUP],
+                    in_=bias_os[groups[0]][:, at * GROUP:(at + 1) * GROUP],
+                )
 
-        for k in range(-X_AHEAD, n_w + 2):
+        for k in range(-X_AHEAD, n_w + 1):
             j_next = x_with.get(k + X_AHEAD)
             banks_next = x_chunks[j_next][1] // PAIR if j_next is not None else 0
+            added = add_at.get(k, ())
+            if ADD_POS == 0:
+                for u in added:
+                    add_bias(u)
             if j_next is not None:
                 transpose_x(j_next)
-            for u in units_at.get(k - 2, ()):
-                transpose_back(u)
+            if SUM_POS == 0 and k in groups_at:
+                sum_a0(groups_at[k])
+            if ADD_POS == 0 and BACK_POS == 0:
+                for u in added:
+                    transpose_back(u)
+            if k == SPREAD_AT:
+                spread_bias_t(N_GROUPS - 1)
             if 0 <= k < n_w:
                 w_quant[k] = quantise(w_grouped[k], [(lo * POWERS * O, hi * POWERS * O) for lo, hi in pieces(k)], "w")
-                if k in x_with:
+                if k in x_with and not (k == 0 and X0_LATE):
                     j = x_with[k]
                     x_quant[j] = quantise(x_grouped[j], [(0, x_chunks[j][1] * POWERS * B)], "x")
             if banks_next > 0:
                 powers_of_x(j_next, 0)
-            if 0 <= k + 1 < n_w:
-                regroup_w(k + 1)
+            if ADD_POS == 1:
+                for u in added:
+                    add_bias(u)
+                if BACK_POS == 0:
+                    for u in added:
+                        transpose_back(u)
             if banks_next > 1:
                 powers_of_x(j_next, 1)
-            if k in groups_at:
+            if 0 <= k + 1 < n_w:
+                regroup_w(k + 1)
+            if k == 0 and X0_LATE:
+                x_quant[0] = quantise(x_grouped[0], [(0, x_chunks[0][1] * POWERS * B)], "x")
+            if SUM_POS == 1 and k in groups_at:
                 sum_a0(groups_at[k])
-                bias_to_sbuf(groups_at[k])
-            for u in units_at.get(k - 1, ()):
-                add_bias(u)
-            for u in units_at.get(k - 2, ()):
-                finish(u)
+            if BACK_POS == 0:
+                for u in added:
+                    finish(u)
             if 0 <= k < n_w:
                 multiply(k)
+            if BACK_POS == 1:
+                for u in added:
+                    transpose_back(u)
+                for u in added:
+                    finish(u)
+            if SUM_POS == 2 and k in groups_at:
+                sum_a0(groups_at[k])
+            if k in groups_at:
+                bias_to_sbuf(groups_at[k])
+            if k == SPREAD_AT:
+                spread_bias_s()
+            for u in units_at.get(k - 1, ()):
+                if u in direct:
+                    finish_direct(u)

@@ -29,7 +29,7 @@ FLOPS = 2 * B * S * POWERS * I * O
 
 W_CHUNKS = (2, 2, 4, 4, 4, 4, 4, 4, 2, 2)
 X_CHUNKS = (2, 2, 4, 4, 4, 4, 4, 4, 4)
-OUT_CHUNKS = (4, 4, 4, 4, 4, 4, 4, 2, 1, 1)
+OUT_CHUNKS = (4, 4, 4, 4, 4, 4, 4, 2, 2)
 LARGEST = 4
 SUM_STEP = (2, 3, 4, 5, 5, 6, 7, 7)
 A0_LOAD = (3, 4, 5, 6, 6, 7, 8, 8)
@@ -38,7 +38,8 @@ ADD_POS = 0
 BACK_POS = 0
 SUM_POS = 1
 X0_LATE = False
-FIN_V = (1, 3, 5)
+FIN_V = (1, 3)
+SUM_COLUMNS = 24
 X_AHEAD = 1
 SPLIT = 3
 X_BANKS = 3
@@ -101,8 +102,9 @@ def tile_modelsingle_kernel(tc, x, taylor_a_0_1, taylor_a_0, out):
             axis=AXIS_X,
             op=ADD,
         )
-        which_s = const.tile([P, GROUP], BF16)
-        nc.vector.tensor_copy(out=which_s[:], in_=which_s_f32[:])
+        which_s = const.tile([P, SUM_COLUMNS], BF16)
+        nc.vector.memset(which_s[:], 0.0)
+        nc.vector.tensor_copy(out=which_s[:, 0:GROUP], in_=which_s_f32[:])
         result = const.tile([P, S * O], F32)
         bias = const.tile([P, S], F32)
         spread = const.tile([P, GROUP * O], F32)
@@ -318,11 +320,11 @@ def tile_modelsingle_kernel(tc, x, taylor_a_0_1, taylor_a_0, out):
             store(u)
 
         def sum_a0(groups):
-            bank = psum.tile([P, 3 * GROUP], F32, tag="bias_os", name="bias_os")
+            bank = psum.tile([P, 2 * SUM_COLUMNS], F32, tag="bias_os", name="bias_os")
             for at, g in enumerate(groups):
                 for r in range(ROWS):
                     nc.tensor.matmul(
-                        out=bank[:, at * GROUP:(at + 1) * GROUP],
+                        out=bank[:, at * SUM_COLUMNS:(at + 1) * SUM_COLUMNS],
                         lhsT=a0_in[g][:, r * O:(r + 1) * O],
                         rhs=which_s[:],
                         start=(r == 0),
@@ -334,7 +336,7 @@ def tile_modelsingle_kernel(tc, x, taylor_a_0_1, taylor_a_0, out):
             for at, g in enumerate(groups):
                 nc.scalar.copy(
                     out=bias[:, g * GROUP:(g + 1) * GROUP],
-                    in_=bias_os[groups[0]][:, at * GROUP:(at + 1) * GROUP],
+                    in_=bias_os[groups[0]][:, at * SUM_COLUMNS:at * SUM_COLUMNS + GROUP],
                 )
 
         for k in range(-X_AHEAD, n_w + 1):

@@ -31,17 +31,24 @@ W_CHUNKS = (2, 2, 4, 4, 4, 4, 4, 4, 2, 2)
 X_CHUNKS = (2, 2, 4, 4, 4, 4, 4, 4, 4)
 OUT_CHUNKS = (4, 4, 4, 4, 4, 4, 4, 2, 2)
 LARGEST = 4
-SUM_STEP = (2, 3, 4, 5, 5, 6, 7, 7)
-A0_LOAD = (3, 4, 5, 6, 6, 7, 8, 8)
+SUM_STEP = (2, 3, 4, 5, 6, 7, 7, 7)
+A0_LOAD = (3, 4, 5, 6, 7, 8, 8, 8)
 SPREAD_AT = 8
 ADD_POS = 0
-BACK_POS = 0
 SUM_POS = 1
 X0_LATE = False
-FIN_V = (1, 3)
+FIN_V = (1, 2, 3)
 SUM_COLUMNS = 24
+STORE_PAIRS = 0
+W_LAST = 0
+X_LOADS = (2, 2, 4, 4, 4, 4, 4, 4, 4)
+X_LOAD = (0, 1, 2, 3, 4, 5, 6, 7, 7)
+QX8 = 1
+S_PRIO = 9
+ADD_LAG = 1
 X_AHEAD = 1
-SPLIT = 3
+SPLIT = 10
+HALVES = 99
 X_BANKS = 3
 SUM_BANKS = 2
 OUT_BANKS = 2
@@ -60,6 +67,7 @@ def tile_modelsingle_kernel(tc, x, taylor_a_0_1, taylor_a_0, out):
     nc = tc.nc
     w_chunks = chunk_list(W_CHUNKS)
     x_chunks = chunk_list(X_CHUNKS)
+    x_loads = chunk_list(X_LOADS)
     n_w = len(w_chunks)
     out_chunks = chunk_list(OUT_CHUNKS)
     direct = [u for u, (first, n) in enumerate(out_chunks) if first >= S - GROUP]
@@ -114,17 +122,19 @@ def tile_modelsingle_kernel(tc, x, taylor_a_0_1, taylor_a_0, out):
         a0_in = {}
         a0_rows = taylor_a_0.rearrange("u s i o -> (u s i) o")
 
-        def load_x(j):
-            first, n = x_chunks[j]
-            x_sb = loads.tile([P, n * I], BF16, name="x_sb%d" % j)
+        def load_x(l):
+            first, n = x_loads[l]
+            x_sb = loads.tile([P, n * I], BF16, name="x_sb%d" % l)
             nc.sync.dma_start(
                 out=x_sb[:], in_=x[:, first:first + n, :].rearrange("b s i -> b (s i)")
             )
-            x_in[j] = x_sb
+            for j, (f, m) in enumerate(x_chunks):
+                if first <= f < first + n:
+                    x_in[j] = x_sb[:, (f - first) * I:(f - first + m) * I]
 
         def pieces(k):
             n = w_chunks[k][1]
-            return [(0, n // 2), (n // 2, n)]
+            return [(0, n // 2), (n // 2, n)] if k < HALVES or k >= n_w - 2 else [(0, n)]
 
         def load_w(k):
             first, n = w_chunks[k]
@@ -149,8 +159,9 @@ def tile_modelsingle_kernel(tc, x, taylor_a_0_1, taylor_a_0, out):
             a0_in[g] = a0_sb
 
         for k in range(n_w):
-            if k in x_with:
-                load_x(x_with[k])
+            for l in range(len(x_loads)):
+                if X_LOAD[l] == k:
+                    load_x(l)
             for g in range(N_GROUPS):
                 if A0_LOAD[g] == k:
                     load_a0(g)
@@ -168,7 +179,7 @@ def tile_modelsingle_kernel(tc, x, taylor_a_0_1, taylor_a_0, out):
 
         def transpose_x(j):
             n = x_chunks[j][1]
-            words = x_in[j][:].bitcast(F32).rearrange("b (s p u) -> b s u p", s=n, u=2)
+            words = x_in[j].bitcast(F32).rearrange("b (s p u) -> b s u p", s=n, u=2)
             for pair in range(n // PAIR):
                 bank = psum.tile([P, 2 * PAIR * B], F32, tag="x_bank", bufs=X_BANKS, name="x_bank")
                 for u in range(2):
@@ -277,6 +288,10 @@ def tile_modelsingle_kernel(tc, x, taylor_a_0_1, taylor_a_0, out):
 
         def store(u):
             first, n = out_chunks[u]
+            if u < STORE_PAIRS:
+                if u % 2 == 0:
+                    return
+                first, n = first - n, 2 * n
             nc.sync.dma_start(
                 out=out[:, first:first + n, :].rearrange("b s o -> b (s o)"),
                 in_=result[:, first * O:(first + n) * O],
@@ -320,7 +335,7 @@ def tile_modelsingle_kernel(tc, x, taylor_a_0_1, taylor_a_0, out):
             store(u)
 
         def sum_a0(groups):
-            bank = psum.tile([P, 2 * SUM_COLUMNS], F32, tag="bias_os", name="bias_os")
+            bank = psum.tile([P, 3 * SUM_COLUMNS], F32, tag="bias_os", name="bias_os")
             for at, g in enumerate(groups):
                 for r in range(ROWS):
                     nc.tensor.matmul(
@@ -343,55 +358,55 @@ def tile_modelsingle_kernel(tc, x, taylor_a_0_1, taylor_a_0, out):
             j_next = x_with.get(k + X_AHEAD)
             banks_next = x_chunks[j_next][1] // PAIR if j_next is not None else 0
             added = add_at.get(k, ())
-            if ADD_POS == 0:
+            early = ADD_POS == 0 and k < S_PRIO
+            if early:
                 for u in added:
                     add_bias(u)
             if j_next is not None:
                 transpose_x(j_next)
             if SUM_POS == 0 and k in groups_at:
                 sum_a0(groups_at[k])
-            if ADD_POS == 0 and BACK_POS == 0:
+            if early:
                 for u in added:
                     transpose_back(u)
-            if k == SPREAD_AT:
-                spread_bias_t(N_GROUPS - 1)
             if 0 <= k < n_w:
                 w_quant[k] = quantise(w_grouped[k], [(lo * POWERS * O, hi * POWERS * O) for lo, hi in pieces(k)], "w")
-                if k in x_with and not (k == 0 and X0_LATE):
+                if k in x_with and not (k == 0 and X0_LATE) and not (k == 8 and QX8):
                     j = x_with[k]
                     x_quant[j] = quantise(x_grouped[j], [(0, x_chunks[j][1] * POWERS * B)], "x")
             if banks_next > 0:
                 powers_of_x(j_next, 0)
-            if ADD_POS == 1:
-                for u in added:
-                    add_bias(u)
-                if BACK_POS == 0:
-                    for u in added:
-                        transpose_back(u)
             if banks_next > 1:
                 powers_of_x(j_next, 1)
+            if not early:
+                for u in added:
+                    add_bias(u)
+            if k == 7 and QX8:
+                x_quant[8] = quantise(x_grouped[8], [(0, x_chunks[8][1] * POWERS * B)], "x")
             if 0 <= k + 1 < n_w:
                 regroup_w(k + 1)
             if k == 0 and X0_LATE:
                 x_quant[0] = quantise(x_grouped[0], [(0, x_chunks[0][1] * POWERS * B)], "x")
             if SUM_POS == 1 and k in groups_at:
                 sum_a0(groups_at[k])
-            if BACK_POS == 0:
+            if early:
                 for u in added:
                     finish(u)
             if 0 <= k < n_w:
                 multiply(k)
-            if BACK_POS == 1:
+            if not early:
                 for u in added:
                     transpose_back(u)
-                for u in added:
-                    finish(u)
             if SUM_POS == 2 and k in groups_at:
                 sum_a0(groups_at[k])
             if k in groups_at:
                 bias_to_sbuf(groups_at[k])
             if k == SPREAD_AT:
+                spread_bias_t(N_GROUPS - 1)
                 spread_bias_s()
+            if not early:
+                for u in added:
+                    finish(u)
             for u in units_at.get(k - 1, ()):
                 if u in direct:
                     finish_direct(u)

@@ -217,9 +217,9 @@ def tile_modelsingle_kernel(tc, x, taylor_a_0_1, taylor_a_0, out):
         def regroup_w(k):
             first, n = w_chunks[k]
             grouped = work.tile([P, LARGEST * POWERS * O * PACK], BF16, align_bytes=64, name="w_grouped")
-            src = w_in[k][:].rearrange("p s (t c r) -> p s c t r", t=PACK, r=4)
+            src = w_in[k][:].rearrange("p s (t c r) -> p s c t r", t=PACK, r=8)
             dst = grouped[:, 0:n * POWERS * O * PACK].rearrange(
-                "p (s c r t) -> p s c t r", s=n, r=4, t=PACK
+                "p (s c r t) -> p s c t r", s=n, r=8, t=PACK
             )
             for lo, hi in pieces(k):
                 nc.vector.tensor_copy(out=dst[:, lo:hi], in_=src[:, lo:hi])

@@ -182,11 +182,11 @@ def tile_modelsingle_kernel(tc, x, taylor_a_0_1, taylor_a_0, out):
             words = x_in[j].bitcast(F32).rearrange("b (s p u) -> b s u p", s=n, u=2)
             for pair in range(n // PAIR):
                 bank = psum.tile([P, 2 * PAIR * B], F32, tag="x_bank", bufs=X_BANKS, name="x_bank")
+                by_half = bank[:].rearrange("p (c u) -> p u c", u=2)
                 for u in range(2):
                     for place in range(PAIR):
-                        col = (u * PAIR + place) * B
                         nc.tensor.transpose(
-                            out=bank[:, col:col + B],
+                            out=by_half[:, u, place * B:(place + 1) * B],
                             in_=words[:, pair * PAIR + place, u, :],
                             identity=ident[:],
                         )
@@ -203,14 +203,14 @@ def tile_modelsingle_kernel(tc, x, taylor_a_0_1, taylor_a_0, out):
                 "p (w h c u) -> p w h c u", w=POWERS, h=n // PAIR, u=2
             )
             nc.scalar.copy(
-                out=as_words[:, 0, pair], in_=bank[:].rearrange("p (u c) -> p c u", u=2)
+                out=as_words[:, 0, pair], in_=bank[:].rearrange("p (c u) -> p c u", u=2)
             )
             as_values = used.rearrange(
                 "p (w h c u e) -> p w h c u e", w=POWERS, h=n // PAIR, u=2, e=2
             )
             nc.scalar.activation(
                 out=as_values[:, 1, pair],
-                in_=bank[:].bitcast(BF16).rearrange("p (u c e) -> p c u e", u=2, e=2),
+                in_=bank[:].bitcast(BF16).rearrange("p (c u e) -> p c u e", u=2, e=2),
                 func=SQUARE,
             )
 

@@ -9,6 +9,7 @@ U32 = mybir.dt.uint32
 U8 = mybir.dt.uint8
 FP8X4 = mybir.dt.float8_e4m3fn_x4
 ADD = mybir.AluOpType.add
+MULT = mybir.AluOpType.mult
 SQUARE = mybir.ActivationFunctionType.Square
 IDENTITY = mybir.ActivationFunctionType.Identity
 AXIS_X = mybir.AxisListType.X
@@ -37,7 +38,9 @@ SPREAD_AT = 8
 ADD_POS = 0
 SUM_POS = 1
 X0_LATE = False
-FIN_V = (1, 2, 3)
+FIN_V = ()
+SQ_V = ((5, 0), (6, 0), (7, 0))
+TX_EARLY = (8,)
 SUM_COLUMNS = 24
 STORE_PAIRS = 0
 W_LAST = 0
@@ -208,11 +211,26 @@ def tile_modelsingle_kernel(tc, x, taylor_a_0_1, taylor_a_0, out):
             as_values = used.rearrange(
                 "p (w h c u e) -> p w h c u e", w=POWERS, h=n // PAIR, u=2, e=2
             )
-            nc.scalar.activation(
-                out=as_values[:, 1, pair],
-                in_=bank[:].bitcast(BF16).rearrange("p (c u e) -> p c u e", u=2, e=2),
-                func=SQUARE,
-            )
+            if (j, pair) not in SQ_V:
+                nc.scalar.activation(
+                    out=as_values[:, 1, pair],
+                    in_=bank[:].bitcast(BF16).rearrange("p (c u e) -> p c u e", u=2, e=2),
+                    func=SQUARE,
+                )
+
+        def square_v(j):
+            n = x_chunks[j][1]
+            for pair in range(n // PAIR):
+                if (j, pair) in SQ_V:
+                    lo = pair * PAIR * B * PACK
+                    hi = lo + PAIR * B * PACK
+                    first_powers = x_grouped[j][:, lo:hi]
+                    nc.vector.tensor_tensor(
+                        out=x_grouped[j][:, lo + n * B * PACK:hi + n * B * PACK],
+                        in0=first_powers,
+                        in1=first_powers,
+                        op=MULT,
+                    )
 
         def regroup_w(k):
             first, n = w_chunks[k]
@@ -362,10 +380,13 @@ def tile_modelsingle_kernel(tc, x, taylor_a_0_1, taylor_a_0, out):
             if early:
                 for u in added:
                     add_bias(u)
-            if j_next is not None:
+            if j_next is not None and j_next not in TX_EARLY:
                 transpose_x(j_next)
+            j_after = x_with.get(k + X_AHEAD + 1)
             if SUM_POS == 0 and k in groups_at:
                 sum_a0(groups_at[k])
+            if k == SPREAD_AT:
+                spread_bias_t(N_GROUPS - 1)
             if early:
                 for u in added:
                     transpose_back(u)
@@ -381,12 +402,16 @@ def tile_modelsingle_kernel(tc, x, taylor_a_0_1, taylor_a_0, out):
             if not early:
                 for u in added:
                     add_bias(u)
+            if j_next is not None:
+                square_v(j_next)
             if k == 7 and QX8:
                 x_quant[8] = quantise(x_grouped[8], [(0, x_chunks[8][1] * POWERS * B)], "x")
             if 0 <= k + 1 < n_w:
                 regroup_w(k + 1)
             if k == 0 and X0_LATE:
                 x_quant[0] = quantise(x_grouped[0], [(0, x_chunks[0][1] * POWERS * B)], "x")
+            if j_after in TX_EARLY:
+                transpose_x(j_after)
             if SUM_POS == 1 and k in groups_at:
                 sum_a0(groups_at[k])
             if early:
@@ -402,7 +427,6 @@ def tile_modelsingle_kernel(tc, x, taylor_a_0_1, taylor_a_0, out):
             if k in groups_at:
                 bias_to_sbuf(groups_at[k])
             if k == SPREAD_AT:
-                spread_bias_t(N_GROUPS - 1)
                 spread_bias_s()
             if not early:
                 for u in added:

@@ -30,28 +30,15 @@ FLOPS = 2 * B * S * POWERS * I * O
 
 W_CHUNKS = (2, 2, 4, 4, 4, 4, 4, 4, 2, 2)
 X_CHUNKS = (2, 2, 4, 4, 4, 4, 4, 4, 4)
-OUT_CHUNKS = (4, 4, 4, 4, 4, 4, 4, 2, 2)
 LARGEST = 4
-SUM_STEP = (2, 3, 4, 5, 6, 7, 7, 7)
-A0_LOAD = (3, 4, 5, 6, 7, 8, 8, 8)
-SPREAD_AT = 8
-ADD_POS = 0
-SUM_POS = 1
-X0_LATE = False
-FIN_V = ()
-SQ_V = ((5, 0), (6, 0), (7, 0))
-TX_EARLY = (8,)
+X_BUFS = 4
+UNITS = (4, 4, 4, 4, 4, 4, 4, 2, 2)
+SUM_LAG = 2
+LAST_SUM_STEP = 7
+SPREAD_STEP = LAST_SUM_STEP + 1
 SUM_COLUMNS = 24
-STORE_PAIRS = 0
-W_LAST = 0
-X_LOADS = (2, 2, 4, 4, 4, 4, 4, 4, 4)
-X_LOAD = (0, 1, 2, 3, 4, 5, 6, 7, 7)
-QX8 = 1
-S_PRIO = 9
-ADD_LAG = 1
-X_AHEAD = 1
-SPLIT = 10
-HALVES = 99
+VECTOR_SQUARES = (6, 7)
+RUN = 8
 X_BANKS = 3
 SUM_BANKS = 2
 OUT_BANKS = 2
@@ -66,34 +53,44 @@ def chunk_list(sizes):
     return chunks
 
 
+def halves(n):
+    return [(0, n // 2), (n // 2, n)]
+
+
 def tile_modelsingle_kernel(tc, x, taylor_a_0_1, taylor_a_0, out):
     nc = tc.nc
     w_chunks = chunk_list(W_CHUNKS)
     x_chunks = chunk_list(X_CHUNKS)
-    x_loads = chunk_list(X_LOADS)
+    units = chunk_list(UNITS)
     n_w = len(w_chunks)
-    out_chunks = chunk_list(OUT_CHUNKS)
-    direct = [u for u, (first, n) in enumerate(out_chunks) if first >= S - GROUP]
-    out_place = {}
-    for u, (first, n) in enumerate(out_chunks):
-        for place in range(n):
-            out_place[first + place] = (u, place)
     w_index = dict((first, k) for k, (first, n) in enumerate(w_chunks))
     x_with = dict((w_index[first], j) for j, (first, n) in enumerate(x_chunks))
+    last_x_step = max(x_with)
     x_place = {}
     for j, (first, n) in enumerate(x_chunks):
         for place in range(n):
             x_place[first + place] = (j, place, n)
-    units_at = {}
-    add_at = {}
-    for u, (first, n) in enumerate(out_chunks):
-        k = [i for i, (f, m) in enumerate(w_chunks) if f < first + n <= f + m][0]
-        units_at.setdefault(k, []).append(u)
-        if u not in direct:
-            add_at.setdefault(max(k, SUM_STEP[u]) + 1, []).append(u)
-    groups_at = {}
+    unit_place = {}
+    for u, (first, n) in enumerate(units):
+        for place in range(n):
+            unit_place[first + place] = (u, place)
+    direct = [u for u, (first, n) in enumerate(units) if first >= S - GROUP]
+    last_group = N_GROUPS - 1
+    sum_steps = {}
+    a0_with = {}
     for g in range(N_GROUPS):
-        groups_at.setdefault(SUM_STEP[g], []).append(g)
+        k = min(g + SUM_LAG, LAST_SUM_STEP)
+        a0_with.setdefault(k + 1, []).append(g)
+        if g != last_group:
+            sum_steps.setdefault(k, []).append(g)
+    add_steps = {}
+    direct_steps = {}
+    for u, (first, n) in enumerate(units):
+        last_chunk = max(k for k in range(n_w) if w_chunks[k][0] < first + n)
+        if u in direct:
+            direct_steps.setdefault(last_chunk + 1, []).append(u)
+        else:
+            add_steps.setdefault(max(last_chunk, min(u + SUM_LAG, LAST_SUM_STEP)) + 1, []).append(u)
 
     with ExitStack() as ctx:
         ctx.enter_context(tc.manual_schedule())
@@ -125,24 +122,18 @@ def tile_modelsingle_kernel(tc, x, taylor_a_0_1, taylor_a_0, out):
         a0_in = {}
         a0_rows = taylor_a_0.rearrange("u s i o -> (u s i) o")
 
-        def load_x(l):
-            first, n = x_loads[l]
-            x_sb = loads.tile([P, n * I], BF16, name="x_sb%d" % l)
+        def load_x(j):
+            first, n = x_chunks[j]
+            x_sb = loads.tile([P, n * I], BF16, name="x_sb%d" % j)
             nc.sync.dma_start(
                 out=x_sb[:], in_=x[:, first:first + n, :].rearrange("b s i -> b (s i)")
             )
-            for j, (f, m) in enumerate(x_chunks):
-                if first <= f < first + n:
-                    x_in[j] = x_sb[:, (f - first) * I:(f - first + m) * I]
-
-        def pieces(k):
-            n = w_chunks[k][1]
-            return [(0, n // 2), (n // 2, n)] if k < HALVES or k >= n_w - 2 else [(0, n)]
+            x_in[j] = x_sb
 
         def load_w(k):
             first, n = w_chunks[k]
             w_sb = loads.tile([P, n, PACK * POWERS * O], BF16, name="w_sb%d" % k)
-            for lo, hi in pieces(k) if k < SPLIT or k == n_w - 1 else [(0, n)]:
+            for lo, hi in halves(n):
                 nc.sync.dma_start(
                     out=w_sb[:, lo:hi],
                     in_=taylor_a_0_1[0, first + lo:first + hi].rearrange(
@@ -162,12 +153,12 @@ def tile_modelsingle_kernel(tc, x, taylor_a_0_1, taylor_a_0, out):
             a0_in[g] = a0_sb
 
         for k in range(n_w):
-            for l in range(len(x_loads)):
-                if X_LOAD[l] == k:
-                    load_x(l)
-            for g in range(N_GROUPS):
-                if A0_LOAD[g] == k:
-                    load_a0(g)
+            if k in x_with and k != last_x_step:
+                load_x(x_with[k])
+            for g in a0_with.get(k, ()):
+                load_a0(g)
+            if k + 1 == last_x_step:
+                load_x(x_with[last_x_step])
             load_w(k)
 
         x_banks = {}
@@ -176,70 +167,60 @@ def tile_modelsingle_kernel(tc, x, taylor_a_0_1, taylor_a_0, out):
         x_quant = {}
         w_quant = {}
         sums = {}
-        bias_os = {}
-        biased_out = {}
+        biased = {}
         out_banks = {}
 
         def transpose_x(j):
             n = x_chunks[j][1]
-            words = x_in[j].bitcast(F32).rearrange("b (s p u) -> b s u p", s=n, u=2)
+            words = x_in[j][:].bitcast(F32).rearrange("b (s p u) -> b s u p", s=n, u=2)
             for pair in range(n // PAIR):
                 bank = psum.tile([P, 2 * PAIR * B], F32, tag="x_bank", bufs=X_BANKS, name="x_bank")
-                by_half = bank[:].rearrange("p (c u) -> p u c", u=2)
+                alternate = bank[:].rearrange("p (c u) -> p u c", u=2)
                 for u in range(2):
                     for place in range(PAIR):
                         nc.tensor.transpose(
-                            out=by_half[:, u, place * B:(place + 1) * B],
+                            out=alternate[:, u, place * B:(place + 1) * B],
                             in_=words[:, pair * PAIR + place, u, :],
                             identity=ident[:],
                         )
                 x_banks[(j, pair)] = bank
 
-        def powers_of_x(j, pair):
+        def powers_of_x(j):
             n = x_chunks[j][1]
-            if pair == 0:
-                grouped = work.tile([P, POWERS * LARGEST * B * PACK], BF16, align_bytes=64, name="x_grouped", bufs=4)
-                x_grouped[j] = grouped
-            used = x_grouped[j][:, 0:POWERS * n * B * PACK]
-            bank = x_banks[(j, pair)]
-            as_words = used.bitcast(F32).rearrange(
-                "p (w h c u) -> p w h c u", w=POWERS, h=n // PAIR, u=2
+            grouped = work.tile(
+                [P, POWERS * LARGEST * B * PACK], BF16, align_bytes=64, name="x_grouped", bufs=X_BUFS
             )
-            nc.scalar.copy(
-                out=as_words[:, 0, pair], in_=bank[:].rearrange("p (c u) -> p c u", u=2)
-            )
-            as_values = used.rearrange(
-                "p (w h c u e) -> p w h c u e", w=POWERS, h=n // PAIR, u=2, e=2
-            )
-            if (j, pair) not in SQ_V:
-                nc.scalar.activation(
-                    out=as_values[:, 1, pair],
-                    in_=bank[:].bitcast(BF16).rearrange("p (c u e) -> p c u e", u=2, e=2),
-                    func=SQUARE,
-                )
-
-        def square_v(j):
-            n = x_chunks[j][1]
+            used = grouped[:, 0:POWERS * n * B * PACK]
+            as_words = used.bitcast(F32).rearrange("p (w h v) -> p w h v", w=POWERS, h=n // PAIR)
+            as_values = used.rearrange("p (w h v) -> p w h v", w=POWERS, h=n // PAIR)
             for pair in range(n // PAIR):
-                if (j, pair) in SQ_V:
-                    lo = pair * PAIR * B * PACK
-                    hi = lo + PAIR * B * PACK
-                    first_powers = x_grouped[j][:, lo:hi]
-                    nc.vector.tensor_tensor(
-                        out=x_grouped[j][:, lo + n * B * PACK:hi + n * B * PACK],
-                        in0=first_powers,
-                        in1=first_powers,
-                        op=MULT,
+                bank = x_banks[(j, pair)]
+                nc.scalar.copy(out=as_words[:, 0, pair], in_=bank[:])
+                if not (j in VECTOR_SQUARES and pair == 0):
+                    nc.scalar.activation(
+                        out=as_values[:, 1, pair], in_=bank[:].bitcast(BF16), func=SQUARE
                     )
+            x_grouped[j] = grouped
+
+        def square_first_pair(j):
+            pair_values = PAIR * B * PACK
+            squares_at = x_chunks[j][1] * B * PACK
+            first_powers = x_grouped[j][:, 0:pair_values]
+            nc.vector.tensor_tensor(
+                out=x_grouped[j][:, squares_at:squares_at + pair_values],
+                in0=first_powers,
+                in1=first_powers,
+                op=MULT,
+            )
 
         def regroup_w(k):
-            first, n = w_chunks[k]
+            n = w_chunks[k][1]
             grouped = work.tile([P, LARGEST * POWERS * O * PACK], BF16, align_bytes=64, name="w_grouped")
-            src = w_in[k][:].rearrange("p s (t c r) -> p s c t r", t=PACK, r=8)
+            src = w_in[k][:].rearrange("p s (t c r) -> p s c t r", t=PACK, r=RUN)
             dst = grouped[:, 0:n * POWERS * O * PACK].rearrange(
-                "p (s c r t) -> p s c t r", s=n, r=8, t=PACK
+                "p (s c r t) -> p s c t r", s=n, r=RUN, t=PACK
             )
-            for lo, hi in pieces(k):
+            for lo, hi in halves(n):
                 nc.vector.tensor_copy(out=dst[:, lo:hi], in_=src[:, lo:hi])
             w_grouped[k] = grouped
 
@@ -254,14 +235,21 @@ def tile_modelsingle_kernel(tc, x, taylor_a_0_1, taylor_a_0, out):
                 )
             return codes, scales
 
+        def quantise_w(k):
+            per_place = POWERS * O
+            windows = [(lo * per_place, hi * per_place) for lo, hi in halves(w_chunks[k][1])]
+            w_quant[k] = quantise(w_grouped[k], windows, "w")
+
+        def quantise_x(j):
+            x_quant[j] = quantise(x_grouped[j], [(0, x_chunks[j][1] * POWERS * B)], "x")
+
         def multiply(k):
             first, n = w_chunks[k]
             w_codes, w_scales = w_quant[k]
             for place in range(n):
-                u, out_at = out_place[first + place]
-                if out_at == 0:
-                    sums[u] = psum.tile([P, LARGEST * B], F32, tag="sums", bufs=SUM_BANKS, name="sums")
-                bank = sums[u]
+                unit, unit_at = unit_place[first + place]
+                if unit_at == 0:
+                    sums[unit] = psum.tile([P, LARGEST * B], F32, tag="sums", bufs=SUM_BANKS, name="sums")
                 j, x_at, x_n = x_place[first + place]
                 x_codes, x_scales = x_quant[j]
                 for w in range(POWERS):
@@ -269,9 +257,9 @@ def tile_modelsingle_kernel(tc, x, taylor_a_0_1, taylor_a_0, out):
                     wc = (place * POWERS + w) * O
                     x_side = (x_codes[:, xc:xc + B].bitcast(FP8X4), x_scales[:, xc:xc + B])
                     w_side = (w_codes[:, wc:wc + O].bitcast(FP8X4), w_scales[:, wc:wc + O])
-                    stationary, moving = (x_side, w_side) if u in direct else (w_side, x_side)
+                    stationary, moving = (x_side, w_side) if unit in direct else (w_side, x_side)
                     nc.tensor.matmul_mx(
-                        out=bank[:, out_at * B:(out_at + 1) * B],
+                        out=sums[unit][:, unit_at * B:(unit_at + 1) * B],
                         lhsT=stationary[0],
                         lhsT_scale=stationary[1],
                         rhs=moving[0],
@@ -280,80 +268,8 @@ def tile_modelsingle_kernel(tc, x, taylor_a_0_1, taylor_a_0, out):
                         stop=(w == POWERS - 1),
                     )
 
-        def add_bias(u):
-            first, n = out_chunks[u]
-            biased = small.tile([P, LARGEST * B], F32, name="biased")
-            for place in range(n):
-                s = first + place
-                nc.scalar.activation(
-                    out=biased[:, place * B:(place + 1) * B],
-                    in_=sums[u][:, place * B:(place + 1) * B],
-                    func=IDENTITY,
-                    bias=bias[:, s:s + 1],
-                )
-            biased_out[u] = biased
-
-        def transpose_back(u):
-            n = out_chunks[u][1]
-            bank = psum.tile([P, LARGEST * O], F32, tag="out_bank", bufs=OUT_BANKS, name="out_bank")
-            for place in range(n):
-                nc.tensor.transpose(
-                    out=bank[:, place * O:(place + 1) * O],
-                    in_=biased_out[u][:, place * B:(place + 1) * B],
-                    identity=ident[:],
-                )
-            out_banks[u] = bank
-
-        def store(u):
-            first, n = out_chunks[u]
-            if u < STORE_PAIRS:
-                if u % 2 == 0:
-                    return
-                first, n = first - n, 2 * n
-            nc.sync.dma_start(
-                out=out[:, first:first + n, :].rearrange("b s o -> b (s o)"),
-                in_=result[:, first * O:(first + n) * O],
-            )
-
-        def finish(u):
-            first, n = out_chunks[u]
-            if u in FIN_V:
-                nc.vector.tensor_copy(
-                    out=result[:, first * O:(first + n) * O], in_=out_banks[u][:, 0:n * O]
-                )
-            else:
-                nc.scalar.copy(
-                    out=result[:, first * O:(first + n) * O], in_=out_banks[u][:, 0:n * O]
-                )
-            store(u)
-
-        def spread_bias_t(g):
-            bank = psum.tile([P, LARGEST * O], F32, tag="out_bank", bufs=OUT_BANKS, name="out_bank")
-            for c in range(GROUP):
-                s = g * GROUP + c
-                nc.tensor.transpose(
-                    out=bank[:, c * O:(c + 1) * O],
-                    in_=bias[:, s:s + 1].to_broadcast([P, P]),
-                    identity=ident[:],
-                )
-            out_banks["spread"] = bank
-
-        def spread_bias_s():
-            nc.scalar.copy(out=spread[:], in_=out_banks["spread"][:])
-
-        def finish_direct(u):
-            first, n = out_chunks[u]
-            lo = first * O - (S - GROUP) * O
-            nc.vector.tensor_tensor(
-                out=result[:, first * O:(first + n) * O],
-                in0=sums[u][:, 0:n * O],
-                in1=spread[:, lo:lo + n * O],
-                op=ADD,
-            )
-            store(u)
-
         def sum_a0(groups):
-            bank = psum.tile([P, 3 * SUM_COLUMNS], F32, tag="bias_os", name="bias_os")
+            bank = psum.tile([P, len(groups) * SUM_COLUMNS], F32, tag="bias_os", name="bias_os")
             for at, g in enumerate(groups):
                 for r in range(ROWS):
                     nc.tensor.matmul(
@@ -363,74 +279,118 @@ def tile_modelsingle_kernel(tc, x, taylor_a_0_1, taylor_a_0, out):
                         start=(r == 0),
                         stop=(r == ROWS - 1),
                     )
-            bias_os[groups[0]] = bank
+            return bank
 
-        def bias_to_sbuf(groups):
+        def bias_to_sbuf(groups, bank):
             for at, g in enumerate(groups):
                 nc.scalar.copy(
                     out=bias[:, g * GROUP:(g + 1) * GROUP],
-                    in_=bias_os[groups[0]][:, at * SUM_COLUMNS:at * SUM_COLUMNS + GROUP],
+                    in_=bank[:, at * SUM_COLUMNS:at * SUM_COLUMNS + GROUP],
                 )
 
-        for k in range(-X_AHEAD, n_w + 1):
-            j_next = x_with.get(k + X_AHEAD)
-            banks_next = x_chunks[j_next][1] // PAIR if j_next is not None else 0
-            added = add_at.get(k, ())
-            early = ADD_POS == 0 and k < S_PRIO
-            if early:
-                for u in added:
-                    add_bias(u)
-            if j_next is not None and j_next not in TX_EARLY:
+        def add_bias(u):
+            first, n = units[u]
+            tile = small.tile([P, LARGEST * B], F32, name="biased")
+            for place in range(n):
+                nc.scalar.activation(
+                    out=tile[:, place * B:(place + 1) * B],
+                    in_=sums[u][:, place * B:(place + 1) * B],
+                    func=IDENTITY,
+                    bias=bias[:, first + place:first + place + 1],
+                )
+            biased[u] = tile
+
+        def transpose_back(u):
+            bank = psum.tile([P, LARGEST * O], F32, tag="out_bank", bufs=OUT_BANKS, name="out_bank")
+            for place in range(units[u][1]):
+                nc.tensor.transpose(
+                    out=bank[:, place * O:(place + 1) * O],
+                    in_=biased[u][:, place * B:(place + 1) * B],
+                    identity=ident[:],
+                )
+            out_banks[u] = bank
+
+        def store(u):
+            first, n = units[u]
+            nc.sync.dma_start(
+                out=out[:, first:first + n, :].rearrange("b s o -> b (s o)"),
+                in_=result[:, first * O:(first + n) * O],
+            )
+
+        def finish(u):
+            first, n = units[u]
+            nc.scalar.copy(
+                out=result[:, first * O:(first + n) * O], in_=out_banks[u][:, 0:n * O]
+            )
+            store(u)
+
+        def transpose_last_bias():
+            bank = psum.tile([P, LARGEST * O], F32, tag="out_bank", bufs=OUT_BANKS, name="out_bank")
+            for c in range(GROUP):
+                s = S - GROUP + c
+                nc.tensor.transpose(
+                    out=bank[:, c * O:(c + 1) * O],
+                    in_=bias[:, s:s + 1].to_broadcast([P, P]),
+                    identity=ident[:],
+                )
+            return bank
+
+        def finish_direct(u):
+            first, n = units[u]
+            lo = (first - (S - GROUP)) * O
+            nc.vector.tensor_tensor(
+                out=result[:, first * O:(first + n) * O],
+                in0=sums[u][:, 0:n * O],
+                in1=spread[:, lo:lo + n * O],
+                op=ADD,
+            )
+            store(u)
+
+        def last_adds():
+            one, other = add_steps[SPREAD_STEP]
+            add_bias(one)
+            transpose_back(one)
+            bank = sum_a0([last_group])
+            add_bias(other)
+            transpose_back(other)
+            finish(one)
+            bias_to_sbuf([last_group], bank)
+            bank = transpose_last_bias()
+            finish(other)
+            nc.scalar.copy(out=spread[:], in_=bank[:])
+
+        for k in range(-1, n_w + 1):
+            added = add_steps.get(k, ()) if k != SPREAD_STEP else ()
+            j_next = x_with.get(k + 1)
+            if k == SPREAD_STEP:
+                last_adds()
+            for u in added:
+                add_bias(u)
+            if j_next is not None and k + 1 != last_x_step:
                 transpose_x(j_next)
-            j_after = x_with.get(k + X_AHEAD + 1)
-            if SUM_POS == 0 and k in groups_at:
-                sum_a0(groups_at[k])
-            if k == SPREAD_AT:
-                spread_bias_t(N_GROUPS - 1)
-            if early:
-                for u in added:
-                    transpose_back(u)
+            for u in added:
+                transpose_back(u)
             if 0 <= k < n_w:
-                w_quant[k] = quantise(w_grouped[k], [(lo * POWERS * O, hi * POWERS * O) for lo, hi in pieces(k)], "w")
-                if k in x_with and not (k == 0 and X0_LATE) and not (k == 8 and QX8):
-                    j = x_with[k]
-                    x_quant[j] = quantise(x_grouped[j], [(0, x_chunks[j][1] * POWERS * B)], "x")
-            if banks_next > 0:
-                powers_of_x(j_next, 0)
-            if banks_next > 1:
-                powers_of_x(j_next, 1)
-            if not early:
-                for u in added:
-                    add_bias(u)
+                quantise_w(k)
+                if k in x_with and k != last_x_step:
+                    quantise_x(x_with[k])
             if j_next is not None:
-                square_v(j_next)
-            if k == 7 and QX8:
-                x_quant[8] = quantise(x_grouped[8], [(0, x_chunks[8][1] * POWERS * B)], "x")
+                powers_of_x(j_next)
+                if j_next in VECTOR_SQUARES:
+                    square_first_pair(j_next)
+            if k + 1 == last_x_step:
+                quantise_x(x_with[last_x_step])
             if 0 <= k + 1 < n_w:
                 regroup_w(k + 1)
-            if k == 0 and X0_LATE:
-                x_quant[0] = quantise(x_grouped[0], [(0, x_chunks[0][1] * POWERS * B)], "x")
-            if j_after in TX_EARLY:
-                transpose_x(j_after)
-            if SUM_POS == 1 and k in groups_at:
-                sum_a0(groups_at[k])
-            if early:
-                for u in added:
-                    finish(u)
+            if k in sum_steps:
+                bias_bank = sum_a0(sum_steps[k])
+            if k + 2 == last_x_step:
+                transpose_x(x_with[last_x_step])
+            for u in added:
+                finish(u)
             if 0 <= k < n_w:
                 multiply(k)
-            if not early:
-                for u in added:
-                    transpose_back(u)
-            if SUM_POS == 2 and k in groups_at:
-                sum_a0(groups_at[k])
-            if k in groups_at:
-                bias_to_sbuf(groups_at[k])
-            if k == SPREAD_AT:
-                spread_bias_s()
-            if not early:
-                for u in added:
-                    finish(u)
-            for u in units_at.get(k - 1, ()):
-                if u in direct:
-                    finish_direct(u)
+            if k in sum_steps:
+                bias_to_sbuf(sum_steps[k], bias_bank)
+            for u in direct_steps.get(k, ()):
+                finish_direct(u)

from contextlib import ExitStack

import concourse.mybir as mybir
from concourse.masks import make_identity

F32 = mybir.dt.float32
BF16 = mybir.dt.bfloat16
U32 = mybir.dt.uint32
U8 = mybir.dt.uint8
FP8X4 = mybir.dt.float8_e4m3fn_x4
ADD = mybir.AluOpType.add
MULT = mybir.AluOpType.mult
SQUARE = mybir.ActivationFunctionType.Square
IDENTITY = mybir.ActivationFunctionType.Identity
AXIS_X = mybir.AxisListType.X

P = 128
B = 128
S = 32
I = 512
POWERS = 2
O = 128
PACK = 4
GROUP = 4
N_GROUPS = S // GROUP
ROWS = GROUP * I // P
PAIR = 2

FLOPS = 2 * B * S * POWERS * I * O

W_CHUNKS = (2, 2, 4, 4, 4, 4, 4, 4, 2, 2)
X_CHUNKS = (2, 2, 4, 4, 4, 4, 4, 4, 4)
LARGEST = 4
X_BUFS = 4
UNITS = (4, 4, 4, 4, 4, 4, 4, 2, 2)
SUM_LAG = 2
LAST_SUM_STEP = 7
SPREAD_STEP = LAST_SUM_STEP + 1
SUM_COLUMNS = 24
VECTOR_SQUARES = (6, 7)
RUN = 8
X_BANKS = 3
SUM_BANKS = 2
OUT_BANKS = 2


def chunk_list(sizes):
    chunks = []
    first = 0
    for n in sizes:
        chunks.append((first, n))
        first += n
    return chunks


def halves(n):
    return [(0, n // 2), (n // 2, n)]


def tile_modelsingle_kernel(tc, x, taylor_a_0_1, taylor_a_0, out):
    nc = tc.nc
    w_chunks = chunk_list(W_CHUNKS)
    x_chunks = chunk_list(X_CHUNKS)
    units = chunk_list(UNITS)
    n_w = len(w_chunks)
    w_index = dict((first, k) for k, (first, n) in enumerate(w_chunks))
    x_with = dict((w_index[first], j) for j, (first, n) in enumerate(x_chunks))
    last_x_step = max(x_with)
    x_place = {}
    for j, (first, n) in enumerate(x_chunks):
        for place in range(n):
            x_place[first + place] = (j, place, n)
    unit_place = {}
    for u, (first, n) in enumerate(units):
        for place in range(n):
            unit_place[first + place] = (u, place)
    direct = [u for u, (first, n) in enumerate(units) if first >= S - GROUP]
    last_group = N_GROUPS - 1
    sum_steps = {}
    a0_with = {}
    for g in range(N_GROUPS):
        k = min(g + SUM_LAG, LAST_SUM_STEP)
        a0_with.setdefault(k + 1, []).append(g)
        if g != last_group:
            sum_steps.setdefault(k, []).append(g)
    add_steps = {}
    direct_steps = {}
    for u, (first, n) in enumerate(units):
        last_chunk = max(k for k in range(n_w) if w_chunks[k][0] < first + n)
        if u in direct:
            direct_steps.setdefault(last_chunk + 1, []).append(u)
        else:
            add_steps.setdefault(max(last_chunk, min(u + SUM_LAG, LAST_SUM_STEP)) + 1, []).append(u)

    with ExitStack() as ctx:
        ctx.enter_context(tc.manual_schedule())
        const = ctx.enter_context(tc.tile_pool(name="const", bufs=1))
        loads = ctx.enter_context(tc.tile_pool(name="loads", bufs=1))
        work = ctx.enter_context(tc.tile_pool(name="work", bufs=3))
        quant = ctx.enter_context(tc.tile_pool(name="quant", bufs=2))
        small = ctx.enter_context(tc.tile_pool(name="small", bufs=3))
        psum = ctx.enter_context(tc.psum_pool(name="psum", bufs=1))

        ident = const.tile([P, P], F32)
        make_identity(nc, ident[:])
        which_s_f32 = const.tile([P, GROUP], F32)
        nc.vector.tensor_reduce(
            out=which_s_f32[:],
            in_=ident[:].rearrange("p (c r) -> p c r", c=GROUP),
            axis=AXIS_X,
            op=ADD,
        )
        which_s = const.tile([P, SUM_COLUMNS], BF16)
        nc.vector.memset(which_s[:], 0.0)
        nc.vector.tensor_copy(out=which_s[:, 0:GROUP], in_=which_s_f32[:])
        result = const.tile([P, S * O], F32)
        bias = const.tile([P, S], F32)
        spread = const.tile([P, GROUP * O], F32)

        x_in = {}
        w_in = {}
        a0_in = {}
        a0_rows = taylor_a_0.rearrange("u s i o -> (u s i) o")

        def load_x(j):
            first, n = x_chunks[j]
            x_sb = loads.tile([P, n * I], BF16, name="x_sb%d" % j)
            nc.sync.dma_start(
                out=x_sb[:], in_=x[:, first:first + n, :].rearrange("b s i -> b (s i)")
            )
            x_in[j] = x_sb

        def load_w(k):
            first, n = w_chunks[k]
            w_sb = loads.tile([P, n, PACK * POWERS * O], BF16, name="w_sb%d" % k)
            for lo, hi in halves(n):
                nc.sync.dma_start(
                    out=w_sb[:, lo:hi],
                    in_=taylor_a_0_1[0, first + lo:first + hi].rearrange(
                        "s (p t) w o -> p s (t w o)", t=PACK
                    ),
                )
            w_in[k] = w_sb

        def load_a0(g):
            a0_sb = loads.tile([P, ROWS * O], BF16, name="a0_sb%d" % g)
            nc.sync.dma_start(
                out=a0_sb[:],
                in_=a0_rows[g * GROUP * I:(g + 1) * GROUP * I, :].rearrange(
                    "(p r) o -> p (r o)", r=ROWS
                ),
            )
            a0_in[g] = a0_sb

        for k in range(n_w):
            if k in x_with and k != last_x_step:
                load_x(x_with[k])
            for g in a0_with.get(k, ()):
                load_a0(g)
            if k + 1 == last_x_step:
                load_x(x_with[last_x_step])
            load_w(k)

        x_banks = {}
        x_grouped = {}
        w_grouped = {}
        x_quant = {}
        w_quant = {}
        sums = {}
        biased = {}
        out_banks = {}

        def transpose_x(j):
            n = x_chunks[j][1]
            words = x_in[j][:].bitcast(F32).rearrange("b (s p u) -> b s u p", s=n, u=2)
            for pair in range(n // PAIR):
                bank = psum.tile([P, 2 * PAIR * B], F32, tag="x_bank", bufs=X_BANKS, name="x_bank")
                alternate = bank[:].rearrange("p (c u) -> p u c", u=2)
                for u in range(2):
                    for place in range(PAIR):
                        nc.tensor.transpose(
                            out=alternate[:, u, place * B:(place + 1) * B],
                            in_=words[:, pair * PAIR + place, u, :],
                            identity=ident[:],
                        )
                x_banks[(j, pair)] = bank

        def powers_of_x(j):
            n = x_chunks[j][1]
            grouped = work.tile(
                [P, POWERS * LARGEST * B * PACK], BF16, align_bytes=64, name="x_grouped", bufs=X_BUFS
            )
            used = grouped[:, 0:POWERS * n * B * PACK]
            as_words = used.bitcast(F32).rearrange("p (w h v) -> p w h v", w=POWERS, h=n // PAIR)
            as_values = used.rearrange("p (w h v) -> p w h v", w=POWERS, h=n // PAIR)
            for pair in range(n // PAIR):
                bank = x_banks[(j, pair)]
                nc.scalar.copy(out=as_words[:, 0, pair], in_=bank[:])
                if not (j in VECTOR_SQUARES and pair == 0):
                    nc.scalar.activation(
                        out=as_values[:, 1, pair], in_=bank[:].bitcast(BF16), func=SQUARE
                    )
            x_grouped[j] = grouped

        def square_first_pair(j):
            pair_values = PAIR * B * PACK
            squares_at = x_chunks[j][1] * B * PACK
            first_powers = x_grouped[j][:, 0:pair_values]
            nc.vector.tensor_tensor(
                out=x_grouped[j][:, squares_at:squares_at + pair_values],
                in0=first_powers,
                in1=first_powers,
                op=MULT,
            )

        def regroup_w(k):
            n = w_chunks[k][1]
            grouped = work.tile([P, LARGEST * POWERS * O * PACK], BF16, align_bytes=64, name="w_grouped")
            src = w_in[k][:].rearrange("p s (t c r) -> p s c t r", t=PACK, r=RUN)
            dst = grouped[:, 0:n * POWERS * O * PACK].rearrange(
                "p (s c r t) -> p s c t r", s=n, r=RUN, t=PACK
            )
            for lo, hi in halves(n):
                nc.vector.tensor_copy(out=dst[:, lo:hi], in_=src[:, lo:hi])
            w_grouped[k] = grouped

        def quantise(grouped, windows, name):
            codes = quant.tile([P, LARGEST * POWERS * O], U32, align_bytes=64, name=name + "_codes")
            scales = quant.tile([P, LARGEST * POWERS * O], U8, align_bytes=64, name=name + "_scales")
            for lo, hi in windows:
                nc.vector.quantize_mx(
                    out=codes[:, lo:hi].bitcast(FP8X4),
                    scales=scales[:, lo:hi],
                    in_=grouped[:, lo * PACK:hi * PACK],
                )
            return codes, scales

        def quantise_w(k):
            per_place = POWERS * O
            windows = [(lo * per_place, hi * per_place) for lo, hi in halves(w_chunks[k][1])]
            w_quant[k] = quantise(w_grouped[k], windows, "w")

        def quantise_x(j):
            x_quant[j] = quantise(x_grouped[j], [(0, x_chunks[j][1] * POWERS * B)], "x")

        def multiply(k):
            first, n = w_chunks[k]
            w_codes, w_scales = w_quant[k]
            for place in range(n):
                unit, unit_at = unit_place[first + place]
                if unit_at == 0:
                    sums[unit] = psum.tile([P, LARGEST * B], F32, tag="sums", bufs=SUM_BANKS, name="sums")
                j, x_at, x_n = x_place[first + place]
                x_codes, x_scales = x_quant[j]
                for w in range(POWERS):
                    xc = (w * x_n + x_at) * B
                    wc = (place * POWERS + w) * O
                    x_side = (x_codes[:, xc:xc + B].bitcast(FP8X4), x_scales[:, xc:xc + B])
                    w_side = (w_codes[:, wc:wc + O].bitcast(FP8X4), w_scales[:, wc:wc + O])
                    stationary, moving = (x_side, w_side) if unit in direct else (w_side, x_side)
                    nc.tensor.matmul_mx(
                        out=sums[unit][:, unit_at * B:(unit_at + 1) * B],
                        lhsT=stationary[0],
                        lhsT_scale=stationary[1],
                        rhs=moving[0],
                        rhs_scale=moving[1],
                        start=(w == 0),
                        stop=(w == POWERS - 1),
                    )

        def sum_a0(groups):
            bank = psum.tile([P, len(groups) * SUM_COLUMNS], F32, tag="bias_os", name="bias_os")
            for at, g in enumerate(groups):
                for r in range(ROWS):
                    nc.tensor.matmul(
                        out=bank[:, at * SUM_COLUMNS:(at + 1) * SUM_COLUMNS],
                        lhsT=a0_in[g][:, r * O:(r + 1) * O],
                        rhs=which_s[:],
                        start=(r == 0),
                        stop=(r == ROWS - 1),
                    )
            return bank

        def bias_to_sbuf(groups, bank):
            for at, g in enumerate(groups):
                nc.scalar.copy(
                    out=bias[:, g * GROUP:(g + 1) * GROUP],
                    in_=bank[:, at * SUM_COLUMNS:at * SUM_COLUMNS + GROUP],
                )

        def add_bias(u):
            first, n = units[u]
            tile = small.tile([P, LARGEST * B], F32, name="biased")
            for place in range(n):
                nc.scalar.activation(
                    out=tile[:, place * B:(place + 1) * B],
                    in_=sums[u][:, place * B:(place + 1) * B],
                    func=IDENTITY,
                    bias=bias[:, first + place:first + place + 1],
                )
            biased[u] = tile

        def transpose_back(u):
            bank = psum.tile([P, LARGEST * O], F32, tag="out_bank", bufs=OUT_BANKS, name="out_bank")
            for place in range(units[u][1]):
                nc.tensor.transpose(
                    out=bank[:, place * O:(place + 1) * O],
                    in_=biased[u][:, place * B:(place + 1) * B],
                    identity=ident[:],
                )
            out_banks[u] = bank

        def store(u):
            first, n = units[u]
            nc.sync.dma_start(
                out=out[:, first:first + n, :].rearrange("b s o -> b (s o)"),
                in_=result[:, first * O:(first + n) * O],
            )

        def finish(u):
            first, n = units[u]
            nc.scalar.copy(
                out=result[:, first * O:(first + n) * O], in_=out_banks[u][:, 0:n * O]
            )
            store(u)

        def transpose_last_bias():
            bank = psum.tile([P, LARGEST * O], F32, tag="out_bank", bufs=OUT_BANKS, name="out_bank")
            for c in range(GROUP):
                s = S - GROUP + c
                nc.tensor.transpose(
                    out=bank[:, c * O:(c + 1) * O],
                    in_=bias[:, s:s + 1].to_broadcast([P, P]),
                    identity=ident[:],
                )
            return bank

        def finish_direct(u):
            first, n = units[u]
            lo = (first - (S - GROUP)) * O
            nc.vector.tensor_tensor(
                out=result[:, first * O:(first + n) * O],
                in0=sums[u][:, 0:n * O],
                in1=spread[:, lo:lo + n * O],
                op=ADD,
            )
            store(u)

        def last_adds():
            one, other = add_steps[SPREAD_STEP]
            add_bias(one)
            transpose_back(one)
            bank = sum_a0([last_group])
            add_bias(other)
            transpose_back(other)
            finish(one)
            bias_to_sbuf([last_group], bank)
            bank = transpose_last_bias()
            finish(other)
            nc.scalar.copy(out=spread[:], in_=bank[:])

        for k in range(-1, n_w + 1):
            added = add_steps.get(k, ()) if k != SPREAD_STEP else ()
            j_next = x_with.get(k + 1)
            if k == SPREAD_STEP:
                last_adds()
            for u in added:
                add_bias(u)
            if j_next is not None and k + 1 != last_x_step:
                transpose_x(j_next)
            for u in added:
                transpose_back(u)
            if 0 <= k < n_w:
                quantise_w(k)
                if k in x_with and k != last_x_step:
                    quantise_x(x_with[k])
            if j_next is not None:
                powers_of_x(j_next)
                if j_next in VECTOR_SQUARES:
                    square_first_pair(j_next)
            if k + 1 == last_x_step:
                quantise_x(x_with[last_x_step])
            if 0 <= k + 1 < n_w:
                regroup_w(k + 1)
            if k in sum_steps:
                bias_bank = sum_a0(sum_steps[k])
            if k + 2 == last_x_step:
                transpose_x(x_with[last_x_step])
            for u in added:
                finish(u)
            if 0 <= k < n_w:
                multiply(k)
            if k in sum_steps:
                bias_to_sbuf(sum_steps[k], bias_bank)
            for u in direct_steps.get(k, ()):
                finish_direct(u)
